import numpy as np
import ml_dtypes


def mxq(x, axis, fmt="e4m3"):
    dtype, down = {"e4m3": (ml_dtypes.float8_e4m3fn, 7), "e5m2": (ml_dtypes.float8_e5m2, 14)}[fmt]
    v = np.moveaxis(np.asarray(x, np.float32).astype(ml_dtypes.bfloat16).astype(np.float64), axis, -1)
    blocks = v.reshape(v.shape[:-1] + (-1, 32))
    amax = np.abs(blocks).max(-1, keepdims=True)
    byte = np.maximum(np.where(amax > 0, np.frexp(amax)[1] - 1 + 127, 0) - down, 1)
    scale = np.exp2(byte - 127.0)
    codes = (blocks / scale).astype(np.float32).astype(dtype).astype(np.float64)
    return np.moveaxis((codes * scale).reshape(v.shape), -1, axis)


WIDE = False


def mx_kscale(k):
    if not WIDE:
        return np.ones(k)
    levels = np.array([10, -10, 5, -5, 0])
    a = np.random.permutation(np.resize(levels, k // 512 * 4)).reshape(k // 512, 4)
    idx = np.arange(k)
    return np.exp2(a[idx // 512, idx % 128 // 32])


BF16 = ml_dtypes.bfloat16


def bf(x):
    return np.asarray(x, np.float32).astype(BF16)


def f64(x):
    return np.asarray(x).astype(np.float64)


E2M1 = np.array([0.0, 0.5, 1.0, 1.5, 2.0, 3.0, 4.0, 6.0, -0.0, -0.5, -1.0, -1.5, -2.0, -3.0, -4.0, -6.0])


def pack_weight(w, fmt):
    k, n = w.shape
    w = f64(bf(w)).reshape(k // 32, 32, n)
    amax = np.abs(w).max(1)
    if fmt == "e4m3":
        byte = np.frexp(amax)[1] - 1 + 127 - 7
    else:
        mant, ex = np.frexp(amax / 6.0)
        byte = np.where(mant > 0.5, ex, ex - 1) + 127
    byte = np.clip(np.where(amax > 0, byte, 1), 1, 254)
    scaled = (w * np.exp2(127.0 - byte)[:, None, :]).reshape(k, n).astype(np.float32)
    by_word = np.ascontiguousarray(scaled.reshape(k // 512, 128, 4, n).transpose(0, 1, 3, 2))
    if fmt == "e4m3":
        words = by_word.astype(ml_dtypes.float8_e4m3fn).view(np.uint8)
    else:
        c = by_word.astype(ml_dtypes.float4_e2m1fn).view(np.uint8) & 0xF
        words = c[..., 0::2] | (c[..., 1::2] << 4)
    return np.ascontiguousarray(words), np.ascontiguousarray(byte.astype(np.uint8).reshape(k // 512, 16, n))


def unpack_weight(words, scales, fmt):
    g, p, n, _ = words.shape
    if fmt == "e4m3":
        vals = np.ascontiguousarray(words).view(ml_dtypes.float8_e4m3fn).astype(np.float64)
    else:
        nib = np.empty((g, p, n, 4), np.uint8)
        nib[..., 0::2] = words & 0xF
        nib[..., 1::2] = words >> 4
        vals = E2M1[nib]
    vals = vals * np.repeat(np.exp2(scales.astype(np.float64) - 127.0), 8, axis=1)[..., None]
    return vals.transpose(0, 1, 3, 2).reshape(g * 512, n)


B, N, C, DIM, H = 4, 1024, 512, 1024, 8
D = DIM // H // 2
LAYER_NUM = 12
LAM_INIT = 0.8 - 0.6 * np.exp(-0.3 * LAYER_NUM)
SCALE = D ** -0.5
FMT = "e4m3"


def split_qk(y):
    y = y.reshape(B, N, H, D, 2)
    return np.moveaxis(y, -1, 2).reshape(B, N, 2 * H, D)


def setup_inputs():
    s = mx_kscale(C)
    ls = 0.45 / D ** 0.25
    x = bf(np.random.standard_normal((B, N, C)) * s)
    Wq = np.random.standard_normal((DIM, C)) / np.sqrt(C) / s
    Wk = np.random.standard_normal((DIM, C)) / np.sqrt(C) / s
    Wq_words, Wq_scales = pack_weight(np.ascontiguousarray(Wq.T), FMT)
    Wk_words, Wk_scales = pack_weight(np.ascontiguousarray(Wk.T), FMT)
    return {"x": x,
            "Wq_words": Wq_words,
            "Wq_scales": Wq_scales,
            "Wk_words": Wk_words,
            "Wk_scales": Wk_scales,
            "lq1": bf(np.random.standard_normal(D) * ls),
            "lq2": bf(np.random.standard_normal(D) * ls),
            "lk1": bf(np.random.standard_normal(D) * ls),
            "lk2": bf(np.random.standard_normal(D) * ls)}


def reference(x, Wq_words, Wq_scales, Wk_words, Wk_scales, lq1, lq2, lk1, lk2):
    xq = mxq(f64(x), 2, "e4m3")
    q = split_qk(xq @ unpack_weight(Wq_words, Wq_scales, FMT)) * SCALE
    k = split_qk(xq @ unpack_weight(Wk_words, Wk_scales, FMT))
    sc = np.stack([(q[:, :, i:i + 1, :] * k).sum(-1) for i in range(2 * H)], axis=2)
    e = np.exp(sc - sc.max(-1, keepdims=True))
    att = e / e.sum(-1, keepdims=True)
    lam = np.exp(np.sum(f64(lq1) * f64(lk1))) - np.exp(np.sum(f64(lq2) * f64(lk2))) + LAM_INIT
    return att[:, :, :H, :H] - lam * att[:, :, H:, H:]

@@ -1,0 +1,220 @@
+import math
+from contextlib import ExitStack
+
+import concourse.mybir as mybir
+from concourse.masks import make_identity
+
+FP8X4 = mybir.dt.float8_e4m3fn_x4
+BF16 = mybir.dt.bfloat16
+F32 = mybir.dt.float32
+I32 = mybir.dt.int32
+U32 = mybir.dt.uint32
+U8 = mybir.dt.uint8
+ALU = mybir.AluOpType
+FUNC = mybir.ActivationFunctionType
+AXIS = mybir.AxisListType
+
+P = 128
+TOKENS = 4096
+K = 512
+DIM = 1024
+HEADS = 8
+D = 64
+ROWS = 2 * HEADS
+BANK = 512
+TILES = TOKENS // P
+D_CHUNK = 16
+STORE_TILES = 8
+SCALE = D ** -0.5
+LAM_INIT = 0.8 - 0.6 * math.exp(-0.3 * 12)
+
+FLOPS = 2 * TOKENS * K * 2 * DIM + 2 * TOKENS * ROWS * ROWS * D
+
+
+def tile_differentialattention_pa_t_kernel(
+    tc, x, Wq_words, Wq_scales, Wk_words, Wk_scales, lq1, lq2, lk1, lk2, out
+):
+    nc = tc.nc
+    x_view = x.flatten_outer_dims().rearrange("(p c) k -> p c k", c=TILES)
+    out_view = out.rearrange("b n a h -> (b n) (a h)").rearrange("(p c) f -> p c f", c=TILES)
+
+    with ExitStack() as ctx:
+        keep = ctx.enter_context(tc.tile_pool(name="keep", bufs=1))
+        stage = ctx.enter_context(tc.tile_pool(name="stage", bufs=2))
+        prods = ctx.enter_context(tc.tile_pool(name="prods", bufs=4))
+        psum_x = ctx.enter_context(tc.psum_pool(name="psum_x", bufs=1))
+        psum_y = ctx.enter_context(tc.psum_pool(name="psum_y", bufs=1))
+        psum_s = ctx.enter_context(tc.psum_pool(name="psum_s", bufs=1))
+
+        ident = keep.tile([P, P], F32)
+        make_identity(nc, ident[:])
+
+        x_sb = keep.tile([P, TILES, K], BF16)
+        w_words = {}
+        w_planes = {}
+        for role in ("q", "k"):
+            w_words[role] = keep.tile([P, DIM], U32, name="w_words_" + role, align_bytes=64)
+            w_planes[role] = keep.tile([P, DIM], U8, name="w_planes_" + role, align_bytes=64)
+            nc.vector.memset(w_planes[role][:].bitcast(I32), 0)
+
+        nc.sync.dma_start(out=x_sb[:, 0:STORE_TILES, :], in_=x_view[:, 0:STORE_TILES, :])
+        for role, words, scales in (("q", Wq_words, Wq_scales), ("k", Wk_words, Wk_scales)):
+            nc.sync.dma_start(
+                out=w_words[role][:].bitcast(I32),
+                in_=words[0].rearrange("p n t -> p (n t)").bitcast(I32),
+            )
+            for quadrant in range(4):
+                nc.sync.dma_start(
+                    out=w_planes[role][32 * quadrant : 32 * quadrant + 4, :].bitcast(I32),
+                    in_=scales[0, 4 * quadrant : 4 * quadrant + 4, :].bitcast(I32),
+                )
+        for first in range(STORE_TILES, TILES, STORE_TILES):
+            nc.sync.dma_start(
+                out=x_sb[:, first : first + STORE_TILES, :],
+                in_=x_view[:, first : first + STORE_TILES, :],
+            )
+
+        lam_vecs = keep.tile([P, 4, D], BF16)
+        for n, vec in enumerate((lq1, lq2, lk1, lk2)):
+            nc.scalar.dma_start(out=lam_vecs[:, n, :], in_=vec.partition_broadcast(P))
+        lam_prod = keep.tile([P, 2, D], F32)
+        nc.vector.tensor_tensor(
+            out=lam_prod[:], in0=lam_vecs[:, 0:2, :], in1=lam_vecs[:, 2:4, :], op=ALU.mult
+        )
+        lam_dots = keep.tile([P, 2], F32)
+        nc.vector.tensor_reduce(out=lam_dots[:], in_=lam_prod[:], axis=AXIS.X, op=ALU.add)
+        lam_exps = keep.tile([P, 2], F32)
+        nc.scalar.activation(out=lam_exps[:], in_=lam_dots[:], func=FUNC.Exp)
+        neg_lam = keep.tile([P, 1], F32)
+        nc.vector.tensor_tensor(
+            out=neg_lam[:], in0=lam_exps[:, 1:2], in1=lam_exps[:, 0:1], op=ALU.subtract
+        )
+        nc.vector.tensor_scalar_add(out=neg_lam[:], in0=neg_lam[:], scalar1=-LAM_INIT)
+
+        x_codes = keep.tile([P, TOKENS], U32, align_bytes=64)
+        x_planes = keep.tile([P, TOKENS], U8, align_bytes=64)
+        x_words = x_sb[:].rearrange("p c k -> p (c k)").bitcast(F32)
+
+        def quantise_two_tiles(pair):
+            flipped = psum_x.tile([P, 2, 2, P], F32)
+            for e in range(2):
+                first_word = (2 * pair + e) * (K // 2)
+                for u in range(2):
+                    nc.tensor.transpose(
+                        flipped[:, e, u, :],
+                        x_words[:, first_word + u : first_word + K // 2 : 2],
+                        ident[:],
+                    )
+            grouped = stage.tile([P, 2 * P * 4], BF16, align_bytes=64)
+            nc.vector.tensor_copy(
+                out=grouped[:].bitcast(F32).rearrange("p (e t u) -> p e t u", e=2, u=2),
+                in_=flipped[:].rearrange("p e u t -> p e t u"),
+            )
+            cols = slice(2 * pair * P, 2 * (pair + 1) * P)
+            nc.vector.quantize_mx(
+                out=x_codes[:, cols].bitcast(FP8X4), scales=x_planes[:, cols], in_=grouped[:]
+            )
+
+        out_sb = keep.tile([P, TILES, HEADS * HEADS], F32)
+
+        def one_tile(c):
+            tokens = slice(c * P, (c + 1) * P)
+            heads = {}
+            for role in ("q", "k"):
+                heads[role] = stage.tile([P, D, ROWS], F32, name="heads_" + role)
+                for half in range(2):
+                    y = psum_y.tile([P, BANK], F32, name="y_%s%d" % (role, half))
+                    cols = slice(half * BANK, (half + 1) * BANK)
+                    nc.tensor.matmul_mx(
+                        out=y[:],
+                        lhsT=x_codes[:, tokens].bitcast(FP8X4),
+                        lhsT_scale=x_planes[:, tokens],
+                        rhs=w_words[role][:, cols].bitcast(FP8X4),
+                        rhs_scale=w_planes[role][:, cols],
+                        start=True,
+                        stop=True,
+                    )
+                    nc.scalar.activation(
+                        out=heads[role][:].rearrange("p d (j h) -> p d j h", j=2)[
+                            :, :, :, 4 * half : 4 * half + 4
+                        ],
+                        in_=y[:].rearrange("p (h d j) -> p d j h", h=4, j=2),
+                        func=FUNC.Copy,
+                        scale=SCALE if role == "q" else 1.0,
+                    )
+
+            sums = [psum_s.tile([P, P], F32, name="sums_%d" % j) for j in range(2)]
+            for d0 in range(0, D, D_CHUNK):
+                prod = prods.tile([P, D_CHUNK, ROWS, ROWS], F32)
+                shape = [P, D_CHUNK, ROWS, ROWS]
+                nc.vector.tensor_tensor(
+                    out=prod[:],
+                    in0=heads["q"][:, d0 : d0 + D_CHUNK, :].unsqueeze(3).to_broadcast(shape),
+                    in1=heads["k"][:, d0 : d0 + D_CHUNK, :].unsqueeze(2).to_broadcast(shape),
+                    op=ALU.mult,
+                )
+                flat = prod[:].rearrange("p d i m -> p d (i m)")
+                for dd in range(D_CHUNK):
+                    for j in range(2):
+                        nc.tensor.matmul(
+                            out=sums[j][:],
+                            lhsT=flat[:, dd, j * P : (j + 1) * P],
+                            rhs=ident[:],
+                            is_transpose=True,
+                            start=(d0 + dd == 0),
+                            stop=(d0 + dd == D - 1),
+                        )
+            sums_sb = stage.tile([P, 2, P], F32)
+            scores = psum_s.tile([P, 2, P], F32)
+            for j in range(2):
+                nc.scalar.copy(out=sums_sb[:, j, :], in_=sums[j][:])
+                nc.tensor.transpose(scores[:, j, :], sums_sb[:, j, :], ident[:])
+            sc = scores[:].rearrange("p j (h m) -> p (j h) m", m=ROWS)
+
+            square = [P, ROWS, ROWS]
+            block = [P, HEADS, HEADS]
+            top = stage.tile([P, ROWS], F32)
+            nc.vector.tensor_reduce(out=top[:], in_=sc, axis=AXIS.X, op=ALU.max)
+            shifted = stage.tile(square, F32)
+            nc.vector.tensor_tensor(
+                out=shifted[:], in0=sc, in1=top[:].unsqueeze(2).to_broadcast(square), op=ALU.subtract
+            )
+            expd = stage.tile(square, F32)
+            nc.scalar.activation(out=expd[:], in_=shifted[:], func=FUNC.Exp)
+            total = stage.tile([P, ROWS], F32)
+            nc.vector.tensor_reduce(out=total[:], in_=expd[:], axis=AXIS.X, op=ALU.add)
+            weight = stage.tile([P, ROWS], F32)
+            nc.vector.reciprocal(out=weight[:], in_=total[:])
+            minus = stage.tile([P, HEADS], F32)
+            nc.vector.tensor_scalar_mul(
+                out=minus[:], in0=weight[:, HEADS:ROWS], scalar1=neg_lam[:, 0:1]
+            )
+            first = stage.tile(block, F32)
+            nc.vector.tensor_tensor(
+                out=first[:],
+                in0=expd[:, 0:HEADS, 0:HEADS],
+                in1=weight[:, 0:HEADS].unsqueeze(2).to_broadcast(block),
+                op=ALU.mult,
+            )
+            second = stage.tile(block, F32)
+            nc.vector.tensor_tensor(
+                out=second[:],
+                in0=expd[:, HEADS:ROWS, HEADS:ROWS],
+                in1=minus[:].unsqueeze(2).to_broadcast(block),
+                op=ALU.mult,
+            )
+            nc.vector.tensor_tensor(
+                out=out_sb[:, c, :].rearrange("p (a h) -> p a h", h=HEADS),
+                in0=first[:],
+                in1=second[:],
+                op=ALU.add,
+            )
+
+        quantise_two_tiles(0)
+        for c in range(TILES):
+            if c % 2 == 0 and c + 2 < TILES:
+                quantise_two_tiles(c // 2 + 1)
+            one_tile(c)
+            if c % STORE_TILES == STORE_TILES - 1:
+                done = slice(c + 1 - STORE_TILES, c + 1)
+                nc.sync.dma_start(out=out_view[:, done, :], in_=out_sb[:, done, :])

@@ -22,11 +22,19 @@ HEADS = 8
 D = 64
 ROWS = 2 * HEADS
 BANK = 512
-TILES = TOKENS // P
-D_CHUNK = 16
-STORE_TILES = 8
 SCALE = D ** -0.5
 LAM_INIT = 0.8 - 0.6 * math.exp(-0.3 * 12)
+
+ROUNDS = 4
+PAIRS_PER_ROUND = 3
+LANE_PER_ROUND = 2
+ROUND_TILES = 2 * PAIRS_PER_ROUND + LANE_PER_ROUND
+PAIRS = ROUNDS * PAIRS_PER_ROUND
+LANE_TILES = ROUNDS * LANE_PER_ROUND
+ARRAY_TOKENS = PAIRS * 2 * P
+PAIRS_PER_BLOCK = 4
+GROUPS = P // 4
+D_CHUNK = 8
 
 FLOPS = 2 * TOKENS * K * 2 * DIM + 2 * TOKENS * ROWS * ROWS * D
 
@@ -35,21 +43,25 @@ def tile_differentialattention_pa_t_kernel(
     tc, x, Wq_words, Wq_scales, Wk_words, Wk_scales, lq1, lq2, lk1, lk2, out
 ):
     nc = tc.nc
-    x_view = x.flatten_outer_dims().rearrange("(p c) k -> p c k", c=TILES)
-    out_view = out.rearrange("b n a h -> (b n) (a h)").rearrange("(p c) f -> p c f", c=TILES)
+    x_flat = x.flatten_outer_dims()
+    out_flat = out.rearrange("b n a h -> (b n) (a h)")
+    x_array = x_flat[0:ARRAY_TOKENS, :].rearrange("(b p s) k -> p b (s k)", p=P, s=2)
+    out_array = out_flat[0:ARRAY_TOKENS, :].rearrange("(B r e) f -> B r (e f)", r=P, e=8)
+    x_lane = x_flat[ARRAY_TOKENS:TOKENS, :].rearrange("(p c) k -> p c k", c=LANE_TILES)
+    out_lane = out_flat[ARRAY_TOKENS:TOKENS, :].rearrange("(p c) f -> p c f", c=LANE_TILES)
 
     with ExitStack() as ctx:
         keep = ctx.enter_context(tc.tile_pool(name="keep", bufs=1))
         stage = ctx.enter_context(tc.tile_pool(name="stage", bufs=2))
         prods = ctx.enter_context(tc.tile_pool(name="prods", bufs=4))
-        psum_x = ctx.enter_context(tc.psum_pool(name="psum_x", bufs=1))
-        psum_y = ctx.enter_context(tc.psum_pool(name="psum_y", bufs=1))
+        psum_y = ctx.enter_context(tc.psum_pool(name="psum_y", bufs=2))
+        psum_t = ctx.enter_context(tc.psum_pool(name="psum_t", bufs=2))
+        psum_c = ctx.enter_context(tc.psum_pool(name="psum_c", bufs=2))
         psum_s = ctx.enter_context(tc.psum_pool(name="psum_s", bufs=1))
 
         ident = keep.tile([P, P], F32)
         make_identity(nc, ident[:])
 
-        x_sb = keep.tile([P, TILES, K], BF16)
         w_words = {}
         w_planes = {}
         for role in ("q", "k"):
@@ -57,7 +69,19 @@ def tile_differentialattention_pa_t_kernel(
             w_planes[role] = keep.tile([P, DIM], U8, name="w_planes_" + role, align_bytes=64)
             nc.vector.memset(w_planes[role][:].bitcast(I32), 0)
 
-        nc.sync.dma_start(out=x_sb[:, 0:STORE_TILES, :], in_=x_view[:, 0:STORE_TILES, :])
+        def load_x(t):
+            x_sb = stage.tile([P, ROUND_TILES, K], BF16, name="x_sb")
+            nc.sync.dma_start(
+                out=x_sb[:, 0 : 2 * PAIRS_PER_ROUND, :].rearrange("p (b s) k -> p b (s k)", s=2),
+                in_=x_array[:, t * PAIRS_PER_ROUND : (t + 1) * PAIRS_PER_ROUND, :],
+            )
+            nc.sync.dma_start(
+                out=x_sb[:, 2 * PAIRS_PER_ROUND : ROUND_TILES, :],
+                in_=x_lane[:, t * LANE_PER_ROUND : (t + 1) * LANE_PER_ROUND, :],
+            )
+            return x_sb
+
+        x_rounds = [load_x(0)]
         for role, words, scales in (("q", Wq_words, Wq_scales), ("k", Wk_words, Wk_scales)):
             nc.sync.dma_start(
                 out=w_words[role][:].bitcast(I32),
@@ -68,11 +92,6 @@ def tile_differentialattention_pa_t_kernel(
                     out=w_planes[role][32 * quadrant : 32 * quadrant + 4, :].bitcast(I32),
                     in_=scales[0, 4 * quadrant : 4 * quadrant + 4, :].bitcast(I32),
                 )
-        for first in range(STORE_TILES, TILES, STORE_TILES):
-            nc.sync.dma_start(
-                out=x_sb[:, first : first + STORE_TILES, :],
-                in_=x_view[:, first : first + STORE_TILES, :],
-            )
 
         lam_vecs = keep.tile([P, 4, D], BF16)
         for n, vec in enumerate((lq1, lq2, lk1, lk2)):
@@ -91,49 +110,163 @@ def tile_differentialattention_pa_t_kernel(
         )
         nc.vector.tensor_scalar_add(out=neg_lam[:], in0=neg_lam[:], scalar1=-LAM_INIT)
 
-        x_codes = keep.tile([P, TOKENS], U32, align_bytes=64)
-        x_planes = keep.tile([P, TOKENS], U8, align_bytes=64)
-        x_words = x_sb[:].rearrange("p c k -> p (c k)").bitcast(F32)
+        queries = [keep.tile([P, P, 2, ROWS], F32, name="queries_%d" % n) for n in range(2)]
+        for n in range(2):
+            nc.gpsimd.memset(queries[n][:], 0.0)
 
-        def quantise_two_tiles(pair):
-            flipped = psum_x.tile([P, 2, 2, P], F32)
-            for e in range(2):
-                first_word = (2 * pair + e) * (K // 2)
-                for u in range(2):
-                    nc.tensor.transpose(
-                        flipped[:, e, u, :],
-                        x_words[:, first_word + u : first_word + K // 2 : 2],
-                        ident[:],
+        def quantise_round(x_sb):
+            codes = stage.tile([P, ROUND_TILES * P], U32, name="codes", align_bytes=64)
+            planes = stage.tile([P, ROUND_TILES * P], U8, name="planes", align_bytes=64)
+            x_words = x_sb[:].rearrange("p c k -> p (c k)").bitcast(F32)
+            for two in range(ROUND_TILES // 2):
+                flipped = psum_t.tile([P, 2, 2, P], F32, tag="flip")
+                for e in range(2):
+                    first_word = (2 * two + e) * (K // 2)
+                    for u in range(2):
+                        nc.tensor.transpose(
+                            flipped[:, e, u, :],
+                            x_words[:, first_word + u : first_word + K // 2 : 2],
+                            ident[:],
+                        )
+                grouped = stage.tile([P, 2 * P * 4], BF16, align_bytes=64)
+                nc.vector.tensor_copy(
+                    out=grouped[:].bitcast(F32).rearrange("p (e t u) -> p e t u", e=2, u=2),
+                    in_=flipped[:].rearrange("p e u t -> p e t u"),
+                )
+                cols = slice(2 * two * P, 2 * (two + 1) * P)
+                nc.vector.quantize_mx(
+                    out=codes[:, cols].bitcast(FP8X4), scales=planes[:, cols], in_=grouped[:]
+                )
+            return codes, planes
+
+        def project(x_mx, slot, role, half):
+            codes, planes = x_mx
+            tokens = slice(slot * P, (slot + 1) * P)
+            cols = slice(half * BANK, (half + 1) * BANK)
+            y = psum_y.tile([P, BANK], F32, name="y")
+            nc.tensor.matmul_mx(
+                out=y[:],
+                lhsT=codes[:, tokens].bitcast(FP8X4),
+                lhsT_scale=planes[:, tokens],
+                rhs=w_words[role][:, cols].bitcast(FP8X4),
+                rhs_scale=w_planes[role][:, cols],
+                start=True,
+                stop=True,
+            )
+            return y
+
+        def array_pair(x_mx, slot, b, probs):
+            rows = {}
+            for role in ("q", "k"):
+                rows[role] = stage.tile([P, ROWS, 2, D], F32, name="rows_" + role)
+            for s in range(2):
+                for role in ("q", "k"):
+                    for half in range(2):
+                        y = project(x_mx, slot + s, role, half)
+                        nc.scalar.activation(
+                            out=rows[role][:].rearrange("p (j h) s d -> p j h s d", j=2)[
+                                :, :, 4 * half : 4 * half + 4, s, :
+                            ],
+                            in_=y[:].rearrange("p (h d j) -> p j h d", h=4, j=2),
+                            func=FUNC.Copy,
+                            scale=SCALE if role == "q" else 1.0,
+                        )
+            keys = stage.tile([P, P, ROWS], F32)
+            for role in ("k", "q"):
+                for four in range(0, ROWS, 4):
+                    flipped = psum_t.tile([P, 4, P], F32, tag="flip")
+                    for n in range(4):
+                        nc.tensor.transpose(
+                            flipped[:, n, :],
+                            rows[role][:, four + n, :, :].rearrange("p s d -> p (s d)"),
+                            ident[:],
+                        )
+                    if role == "k":
+                        nc.scalar.copy(
+                            out=keys[:, :, four : four + 4],
+                            in_=flipped[:].rearrange("r n p -> r p n"),
+                        )
+                    else:
+                        for s in range(2):
+                            own = slice(D * s, D * (s + 1))
+                            nc.scalar.copy(
+                                out=queries[b % 2][own, :, s, four : four + 4],
+                                in_=flipped[own, :, :].rearrange("r n p -> r p n"),
+                            )
+            scores = stage.tile([P, GROUPS, ROWS], F32)
+            for first in range(0, GROUPS, 8):
+                cross = psum_c.tile([P, 8, 4, ROWS], F32)
+                for n in range(8):
+                    four_p = slice(4 * (first + n), 4 * (first + n + 1))
+                    nc.tensor.matmul(
+                        out=cross[:, n, :, :],
+                        lhsT=queries[b % 2][:, four_p, :, :].rearrange("r p s i -> r (p s i)"),
+                        rhs=keys[:, four_p, :],
+                        start=True,
+                        stop=True,
                     )
-            grouped = stage.tile([P, 2 * P * 4], BF16, align_bytes=64)
-            nc.vector.tensor_copy(
-                out=grouped[:].bitcast(F32).rearrange("p (e t u) -> p e t u", e=2, u=2),
-                in_=flipped[:].rearrange("p e u t -> p e t u"),
+                for g in range(4):
+                    quarter = slice(32 * g, 32 * (g + 1))
+                    nc.scalar.copy(
+                        out=scores[quarter, first : first + 8, :], in_=cross[quarter, :, g, :]
+                    )
+            full = [P, GROUPS, ROWS]
+            top = stage.tile([P, GROUPS], F32)
+            nc.vector.tensor_reduce(out=top[:], in_=scores[:], axis=AXIS.X, op=ALU.max)
+            nc.vector.tensor_tensor(
+                out=scores[:],
+                in0=scores[:],
+                in1=top[:].unsqueeze(2).to_broadcast(full),
+                op=ALU.subtract,
             )
-            cols = slice(2 * pair * P, 2 * (pair + 1) * P)
-            nc.vector.quantize_mx(
-                out=x_codes[:, cols].bitcast(FP8X4), scales=x_planes[:, cols], in_=grouped[:]
+            nc.scalar.activation(out=scores[:], in_=scores[:], func=FUNC.Exp)
+            total = stage.tile([P, GROUPS], F32)
+            nc.vector.tensor_reduce(out=total[:], in_=scores[:], axis=AXIS.X, op=ALU.add)
+            weight = stage.tile([P, GROUPS], F32)
+            nc.vector.reciprocal(out=weight[:], in_=total[:])
+            place = (b % PAIRS_PER_BLOCK) * GROUPS
+            nc.vector.tensor_tensor(
+                out=probs[:, :, place : place + GROUPS],
+                in0=scores[:].rearrange("r G m -> r m G"),
+                in1=weight[:].unsqueeze(1).to_broadcast([P, ROWS, GROUPS]),
+                op=ALU.mult,
             )
 
-        out_sb = keep.tile([P, TILES, HEADS * HEADS], F32)
+        def array_block(block, probs):
+            second = stage.tile([P, 8, HEADS, HEADS], F32)
+            result = stage.tile([P, 8, HEADS, HEADS], F32)
+            for j in (1, 0):
+                for four in range(0, HEADS, 4):
+                    back = psum_t.tile([P, 4, 8, 2, HEADS], F32, tag="flip")
+                    for n in range(4):
+                        nc.tensor.transpose(
+                            back[:, n, :, :, :].rearrange("r e j a -> r (e j a)"),
+                            probs[:, HEADS * j + four + n, :],
+                            ident[:],
+                        )
+                    wanted = back[:, :, :, j, :].rearrange("r h e a -> r e a h")
+                    if j == 1:
+                        nc.scalar.activation(
+                            out=second[:, :, :, four : four + 4],
+                            in_=wanted,
+                            func=FUNC.Copy,
+                            scale=neg_lam[:, 0:1],
+                        )
+                    else:
+                        nc.vector.tensor_tensor(
+                            out=result[:, :, :, four : four + 4],
+                            in0=wanted,
+                            in1=second[:, :, :, four : four + 4],
+                            op=ALU.add,
+                        )
+            nc.sync.dma_start(out=out_array[block], in_=result[:].rearrange("r e a h -> r (e a h)"))
 
-        def one_tile(c):
-            tokens = slice(c * P, (c + 1) * P)
+        def lane_tile(x_mx, slot, result):
             heads = {}
             for role in ("q", "k"):
                 heads[role] = stage.tile([P, D, ROWS], F32, name="heads_" + role)
                 for half in range(2):
-                    y = psum_y.tile([P, BANK], F32, name="y_%s%d" % (role, half))
-                    cols = slice(half * BANK, (half + 1) * BANK)
-                    nc.tensor.matmul_mx(
-                        out=y[:],
-                        lhsT=x_codes[:, tokens].bitcast(FP8X4),
-                        lhsT_scale=x_planes[:, tokens],
-                        rhs=w_words[role][:, cols].bitcast(FP8X4),
-                        rhs_scale=w_planes[role][:, cols],
-                        start=True,
-                        stop=True,
-                    )
+                    y = project(x_mx, slot, role, half)
                     nc.scalar.activation(
                         out=heads[role][:].rearrange("p d (j h) -> p d j h", j=2)[
                             :, :, :, 4 * half : 4 * half + 4
@@ -142,11 +275,10 @@ def tile_differentialattention_pa_t_kernel(
                         func=FUNC.Copy,
                         scale=SCALE if role == "q" else 1.0,
                     )
-
             sums = [psum_s.tile([P, P], F32, name="sums_%d" % j) for j in range(2)]
+            shape = [P, D_CHUNK, ROWS, ROWS]
             for d0 in range(0, D, D_CHUNK):
-                prod = prods.tile([P, D_CHUNK, ROWS, ROWS], F32)
-                shape = [P, D_CHUNK, ROWS, ROWS]
+                prod = prods.tile(shape, F32)
                 nc.vector.tensor_tensor(
                     out=prod[:],
                     in0=heads["q"][:, d0 : d0 + D_CHUNK, :].unsqueeze(3).to_broadcast(shape),
@@ -165,56 +297,65 @@ def tile_differentialattention_pa_t_kernel(
                             stop=(d0 + dd == D - 1),
                         )
             sums_sb = stage.tile([P, 2, P], F32)
-            scores = psum_s.tile([P, 2, P], F32)
+            back = psum_t.tile([P, 2, P], F32, tag="flip")
             for j in range(2):
                 nc.scalar.copy(out=sums_sb[:, j, :], in_=sums[j][:])
-                nc.tensor.transpose(scores[:, j, :], sums_sb[:, j, :], ident[:])
-            sc = scores[:].rearrange("p j (h m) -> p (j h) m", m=ROWS)
+                nc.tensor.transpose(back[:, j, :], sums_sb[:, j, :], ident[:])
+            sc = back[:].rearrange("p j (h m) -> p (j h) m", m=ROWS)
 
             square = [P, ROWS, ROWS]
-            block = [P, HEADS, HEADS]
-            top = stage.tile([P, ROWS], F32)
-            nc.vector.tensor_reduce(out=top[:], in_=sc, axis=AXIS.X, op=ALU.max)
-            shifted = stage.tile(square, F32)
-            nc.vector.tensor_tensor(
-                out=shifted[:], in0=sc, in1=top[:].unsqueeze(2).to_broadcast(square), op=ALU.subtract
-            )
+            corner = [P, HEADS, HEADS]
+            peak = stage.tile([P, ROWS], F32)
+            nc.vector.tensor_reduce(out=peak[:], in_=sc, axis=AXIS.X, op=ALU.max)
             expd = stage.tile(square, F32)
-            nc.scalar.activation(out=expd[:], in_=shifted[:], func=FUNC.Exp)
-            total = stage.tile([P, ROWS], F32)
-            nc.vector.tensor_reduce(out=total[:], in_=expd[:], axis=AXIS.X, op=ALU.add)
-            weight = stage.tile([P, ROWS], F32)
-            nc.vector.reciprocal(out=weight[:], in_=total[:])
+            nc.vector.tensor_tensor(
+                out=expd[:], in0=sc, in1=peak[:].unsqueeze(2).to_broadcast(square), op=ALU.subtract
+            )
+            nc.scalar.activation(out=expd[:], in_=expd[:], func=FUNC.Exp)
+            norm = stage.tile([P, ROWS], F32)
+            nc.vector.tensor_reduce(out=norm[:], in_=expd[:], axis=AXIS.X, op=ALU.add)
+            inverse = stage.tile([P, ROWS], F32)
+            nc.vector.reciprocal(out=inverse[:], in_=norm[:])
             minus = stage.tile([P, HEADS], F32)
             nc.vector.tensor_scalar_mul(
-                out=minus[:], in0=weight[:, HEADS:ROWS], scalar1=neg_lam[:, 0:1]
+                out=minus[:], in0=inverse[:, HEADS:ROWS], scalar1=neg_lam[:, 0:1]
             )
-            first = stage.tile(block, F32)
+            upper = stage.tile(corner, F32)
             nc.vector.tensor_tensor(
-                out=first[:],
+                out=upper[:],
                 in0=expd[:, 0:HEADS, 0:HEADS],
-                in1=weight[:, 0:HEADS].unsqueeze(2).to_broadcast(block),
+                in1=inverse[:, 0:HEADS].unsqueeze(2).to_broadcast(corner),
                 op=ALU.mult,
             )
-            second = stage.tile(block, F32)
+            lower = stage.tile(corner, F32)
             nc.vector.tensor_tensor(
-                out=second[:],
+                out=lower[:],
                 in0=expd[:, HEADS:ROWS, HEADS:ROWS],
-                in1=minus[:].unsqueeze(2).to_broadcast(block),
+                in1=minus[:].unsqueeze(2).to_broadcast(corner),
                 op=ALU.mult,
             )
             nc.vector.tensor_tensor(
-                out=out_sb[:, c, :].rearrange("p (a h) -> p a h", h=HEADS),
-                in0=first[:],
-                in1=second[:],
+                out=result.rearrange("p (a h) -> p a h", h=HEADS),
+                in0=upper[:],
+                in1=lower[:],
                 op=ALU.add,
             )
 
-        quantise_two_tiles(0)
-        for c in range(TILES):
-            if c % 2 == 0 and c + 2 < TILES:
-                quantise_two_tiles(c // 2 + 1)
-            one_tile(c)
-            if c % STORE_TILES == STORE_TILES - 1:
-                done = slice(c + 1 - STORE_TILES, c + 1)
-                nc.sync.dma_start(out=out_view[:, done, :], in_=out_sb[:, done, :])
+        probs = None
+        for t in range(ROUNDS):
+            if t + 1 < ROUNDS:
+                x_rounds.append(load_x(t + 1))
+            x_mx = quantise_round(x_rounds[t])
+            lane_out = stage.tile([P, LANE_PER_ROUND, HEADS * HEADS], F32)
+            for n in range(PAIRS_PER_ROUND):
+                b = t * PAIRS_PER_ROUND + n
+                if b % PAIRS_PER_BLOCK == 0:
+                    probs = stage.tile([P, ROWS, P], F32, name="probs")
+                array_pair(x_mx, 2 * n, b, probs)
+                if b % PAIRS_PER_BLOCK == PAIRS_PER_BLOCK - 1:
+                    array_block(b // PAIRS_PER_BLOCK, probs)
+                if n < LANE_PER_ROUND:
+                    lane_tile(x_mx, 2 * PAIRS_PER_ROUND + n, lane_out[:, n, :])
+            nc.sync.dma_start(
+                out=out_lane[:, t * LANE_PER_ROUND : (t + 1) * LANE_PER_ROUND, :], in_=lane_out[:]
+            )

@@ -25,16 +25,18 @@ BANK = 512
 SCALE = D ** -0.5
 LAM_INIT = 0.8 - 0.6 * math.exp(-0.3 * 12)
 
-ROUNDS = 4
-PAIRS_PER_ROUND = 3
-LANE_PER_ROUND = 2
-ROUND_TILES = 2 * PAIRS_PER_ROUND + LANE_PER_ROUND
-PAIRS = ROUNDS * PAIRS_PER_ROUND
-LANE_TILES = ROUNDS * LANE_PER_ROUND
+TILES = TOKENS // P
+PAIRS = 12
+LANE_TILES = TILES - 2 * PAIRS
 ARRAY_TOKENS = PAIRS * 2 * P
 PAIRS_PER_BLOCK = 4
+PAIRS_PER_LOAD = 3
 GROUPS = P // 4
 D_CHUNK = 8
+LANE_CHUNKS = LANE_TILES * (D // D_CHUNK)
+LANE_AHEAD = 4
+STEPS = PAIRS + 2
+QUARTERS = 4 * STEPS
 
 FLOPS = 2 * TOKENS * K * 2 * DIM + 2 * TOKENS * ROWS * ROWS * D
 
@@ -62,6 +64,7 @@ def tile_differentialattention_pa_t_kernel(
         ident = keep.tile([P, P], F32)
         make_identity(nc, ident[:])
 
+        x_sb = keep.tile([P, TILES, K], BF16)
         w_words = {}
         w_planes = {}
         for role in ("q", "k"):
@@ -69,19 +72,15 @@ def tile_differentialattention_pa_t_kernel(
             w_planes[role] = keep.tile([P, DIM], U8, name="w_planes_" + role, align_bytes=64)
             nc.vector.memset(w_planes[role][:].bitcast(I32), 0)
 
-        def load_x(t):
-            x_sb = stage.tile([P, ROUND_TILES, K], BF16, name="x_sb")
+        def load_pairs(first_pair):
+            pairs = slice(first_pair, first_pair + PAIRS_PER_LOAD)
+            tiles = slice(2 * first_pair, 2 * (first_pair + PAIRS_PER_LOAD))
             nc.sync.dma_start(
-                out=x_sb[:, 0 : 2 * PAIRS_PER_ROUND, :].rearrange("p (b s) k -> p b (s k)", s=2),
-                in_=x_array[:, t * PAIRS_PER_ROUND : (t + 1) * PAIRS_PER_ROUND, :],
+                out=x_sb[:, tiles, :].rearrange("p (b s) k -> p b (s k)", s=2),
+                in_=x_array[:, pairs, :],
             )
-            nc.sync.dma_start(
-                out=x_sb[:, 2 * PAIRS_PER_ROUND : ROUND_TILES, :],
-                in_=x_lane[:, t * LANE_PER_ROUND : (t + 1) * LANE_PER_ROUND, :],
-            )
-            return x_sb
 
-        x_rounds = [load_x(0)]
+        load_pairs(0)
         for role, words, scales in (("q", Wq_words, Wq_scales), ("k", Wk_words, Wk_scales)):
             nc.sync.dma_start(
                 out=w_words[role][:].bitcast(I32),
@@ -92,6 +91,9 @@ def tile_differentialattention_pa_t_kernel(
                     out=w_planes[role][32 * quadrant : 32 * quadrant + 4, :].bitcast(I32),
                     in_=scales[0, 4 * quadrant : 4 * quadrant + 4, :].bitcast(I32),
                 )
+        nc.sync.dma_start(out=x_sb[:, 2 * PAIRS : TILES, :], in_=x_lane)
+        for first_pair in range(PAIRS_PER_LOAD, PAIRS, PAIRS_PER_LOAD):
+            load_pairs(first_pair)
 
         lam_vecs = keep.tile([P, 4, D], BF16)
         for n, vec in enumerate((lq1, lq2, lk1, lk2)):
@@ -114,40 +116,38 @@ def tile_differentialattention_pa_t_kernel(
         for n in range(2):
             nc.gpsimd.memset(queries[n][:], 0.0)
 
-        def quantise_round(x_sb):
-            codes = stage.tile([P, ROUND_TILES * P], U32, name="codes", align_bytes=64)
-            planes = stage.tile([P, ROUND_TILES * P], U8, name="planes", align_bytes=64)
-            x_words = x_sb[:].rearrange("p c k -> p (c k)").bitcast(F32)
-            for two in range(ROUND_TILES // 2):
-                flipped = psum_t.tile([P, 2, 2, P], F32, tag="flip")
-                for e in range(2):
-                    first_word = (2 * two + e) * (K // 2)
-                    for u in range(2):
-                        nc.tensor.transpose(
-                            flipped[:, e, u, :],
-                            x_words[:, first_word + u : first_word + K // 2 : 2],
-                            ident[:],
-                        )
-                grouped = stage.tile([P, 2 * P * 4], BF16, align_bytes=64)
-                nc.vector.tensor_copy(
-                    out=grouped[:].bitcast(F32).rearrange("p (e t u) -> p e t u", e=2, u=2),
-                    in_=flipped[:].rearrange("p e u t -> p e t u"),
-                )
-                cols = slice(2 * two * P, 2 * (two + 1) * P)
-                nc.vector.quantize_mx(
-                    out=codes[:, cols].bitcast(FP8X4), scales=planes[:, cols], in_=grouped[:]
-                )
-            return codes, planes
+        x_codes = keep.tile([P, TOKENS], U32, align_bytes=64)
+        x_planes = keep.tile([P, TOKENS], U8, align_bytes=64)
+        x_words = x_sb[:].rearrange("p c k -> p (c k)").bitcast(F32)
 
-        def project(x_mx, slot, role, half):
-            codes, planes = x_mx
-            tokens = slice(slot * P, (slot + 1) * P)
+        def quantise_two_tiles(two):
+            flipped = psum_t.tile([P, 2, 2, P], F32, tag="flip")
+            for e in range(2):
+                first_word = (2 * two + e) * (K // 2)
+                for u in range(2):
+                    nc.tensor.transpose(
+                        flipped[:, e, u, :],
+                        x_words[:, first_word + u : first_word + K // 2 : 2],
+                        ident[:],
+                    )
+            grouped = stage.tile([P, 2 * P * 4], BF16, align_bytes=64)
+            nc.vector.tensor_copy(
+                out=grouped[:].bitcast(F32).rearrange("p (e t u) -> p e t u", e=2, u=2),
+                in_=flipped[:].rearrange("p e u t -> p e t u"),
+            )
+            cols = slice(2 * two * P, 2 * (two + 1) * P)
+            nc.vector.quantize_mx(
+                out=x_codes[:, cols].bitcast(FP8X4), scales=x_planes[:, cols], in_=grouped[:]
+            )
+
+        def project(c, role, half):
+            tokens = slice(c * P, (c + 1) * P)
             cols = slice(half * BANK, (half + 1) * BANK)
             y = psum_y.tile([P, BANK], F32, name="y")
             nc.tensor.matmul_mx(
                 out=y[:],
-                lhsT=codes[:, tokens].bitcast(FP8X4),
-                lhsT_scale=planes[:, tokens],
+                lhsT=x_codes[:, tokens].bitcast(FP8X4),
+                lhsT_scale=x_planes[:, tokens],
                 rhs=w_words[role][:, cols].bitcast(FP8X4),
                 rhs_scale=w_planes[role][:, cols],
                 start=True,
@@ -155,93 +155,107 @@ def tile_differentialattention_pa_t_kernel(
             )
             return y
 
-        def array_pair(x_mx, slot, b, probs):
-            rows = {}
-            for role in ("q", "k"):
-                rows[role] = stage.tile([P, ROWS, 2, D], F32, name="rows_" + role)
-            for s in range(2):
-                for role in ("q", "k"):
-                    for half in range(2):
-                        y = project(x_mx, slot + s, role, half)
-                        nc.scalar.activation(
-                            out=rows[role][:].rearrange("p (j h) s d -> p j h s d", j=2)[
-                                :, :, 4 * half : 4 * half + 4, s, :
-                            ],
-                            in_=y[:].rearrange("p (h d j) -> p j h d", h=4, j=2),
-                            func=FUNC.Copy,
-                            scale=SCALE if role == "q" else 1.0,
-                        )
-            keys = stage.tile([P, P, ROWS], F32)
-            for role in ("k", "q"):
-                for four in range(0, ROWS, 4):
-                    flipped = psum_t.tile([P, 4, P], F32, tag="flip")
-                    for n in range(4):
-                        nc.tensor.transpose(
-                            flipped[:, n, :],
-                            rows[role][:, four + n, :, :].rearrange("p s d -> p (s d)"),
-                            ident[:],
-                        )
-                    if role == "k":
-                        nc.scalar.copy(
-                            out=keys[:, :, four : four + 4],
-                            in_=flipped[:].rearrange("r n p -> r p n"),
-                        )
-                    else:
-                        for s in range(2):
-                            own = slice(D * s, D * (s + 1))
-                            nc.scalar.copy(
-                                out=queries[b % 2][own, :, s, four : four + 4],
-                                in_=flipped[own, :, :].rearrange("r n p -> r p n"),
-                            )
-            scores = stage.tile([P, GROUPS, ROWS], F32)
-            for first in range(0, GROUPS, 8):
-                cross = psum_c.tile([P, 8, 4, ROWS], F32)
-                for n in range(8):
-                    four_p = slice(4 * (first + n), 4 * (first + n + 1))
-                    nc.tensor.matmul(
-                        out=cross[:, n, :, :],
-                        lhsT=queries[b % 2][:, four_p, :, :].rearrange("r p s i -> r (p s i)"),
-                        rhs=keys[:, four_p, :],
-                        start=True,
-                        stop=True,
+        rows = {}
+        keys = {}
+        scores = {}
+        probs = {}
+
+        def project_quarter(b, quarter):
+            s, role = quarter // 2, ("q", "k")[quarter % 2]
+            if s == 0:
+                rows[b, role] = stage.tile([P, ROWS, 2, D], F32, name="rows_" + role)
+            for half in range(2):
+                y = project(2 * b + s, role, half)
+                nc.scalar.activation(
+                    out=rows[b, role][:].rearrange("p (j h) s d -> p j h s d", j=2)[
+                        :, :, 4 * half : 4 * half + 4, s, :
+                    ],
+                    in_=y[:].rearrange("p (h d j) -> p j h d", h=4, j=2),
+                    func=FUNC.Copy,
+                    scale=SCALE if role == "q" else 1.0,
+                )
+
+        def flip_quarter(b, quarter):
+            role = ("k", "q")[quarter // 2]
+            if quarter == 0:
+                keys[b] = stage.tile([P, P, ROWS], F32, name="keys")
+            for four in range(8 * (quarter % 2), 8 * (quarter % 2) + 8, 4):
+                flipped = psum_t.tile([P, 4, P], F32, tag="flip")
+                for n in range(4):
+                    nc.tensor.transpose(
+                        flipped[:, n, :],
+                        rows[b, role][:, four + n, :, :].rearrange("p s d -> p (s d)"),
+                        ident[:],
                     )
-                for g in range(4):
-                    quarter = slice(32 * g, 32 * (g + 1))
+                if role == "k":
                     nc.scalar.copy(
-                        out=scores[quarter, first : first + 8, :], in_=cross[quarter, :, g, :]
+                        out=keys[b][:, :, four : four + 4],
+                        in_=flipped[:].rearrange("r n p -> r p n"),
                     )
-            full = [P, GROUPS, ROWS]
+                else:
+                    for s in range(2):
+                        own = slice(D * s, D * (s + 1))
+                        nc.scalar.copy(
+                            out=queries[b % 2][own, :, s, four : four + 4],
+                            in_=flipped[own, :, :].rearrange("r n p -> r p n"),
+                        )
+
+        def score_quarter(b, quarter):
+            if quarter == 0:
+                scores[b] = stage.tile([P, GROUPS, ROWS], F32, name="scores")
+            first = 8 * quarter
+            cross = psum_c.tile([P, 8, 4, ROWS], F32)
+            for n in range(8):
+                four_p = slice(4 * (first + n), 4 * (first + n + 1))
+                nc.tensor.matmul(
+                    out=cross[:, n, :, :],
+                    lhsT=queries[b % 2][:, four_p, :, :].rearrange("r p s i -> r (p s i)"),
+                    rhs=keys[b][:, four_p, :],
+                    start=True,
+                    stop=True,
+                )
+            for g in range(4):
+                quadrant = slice(32 * g, 32 * (g + 1))
+                nc.scalar.copy(
+                    out=scores[b][quadrant, first : first + 8, :], in_=cross[quadrant, :, g, :]
+                )
+
+        def softmax_pair(b):
+            block = b // PAIRS_PER_BLOCK
+            if b % PAIRS_PER_BLOCK == 0:
+                probs[block] = keep.tile([P, ROWS, P], F32, name="probs")
+            sc = scores[b]
             top = stage.tile([P, GROUPS], F32)
-            nc.vector.tensor_reduce(out=top[:], in_=scores[:], axis=AXIS.X, op=ALU.max)
+            nc.vector.tensor_reduce(out=top[:], in_=sc[:], axis=AXIS.X, op=ALU.max)
             nc.vector.tensor_tensor(
-                out=scores[:],
-                in0=scores[:],
-                in1=top[:].unsqueeze(2).to_broadcast(full),
+                out=sc[:],
+                in0=sc[:],
+                in1=top[:].unsqueeze(2).to_broadcast([P, GROUPS, ROWS]),
                 op=ALU.subtract,
             )
-            nc.scalar.activation(out=scores[:], in_=scores[:], func=FUNC.Exp)
+            nc.scalar.activation(out=sc[:], in_=sc[:], func=FUNC.Exp)
             total = stage.tile([P, GROUPS], F32)
-            nc.vector.tensor_reduce(out=total[:], in_=scores[:], axis=AXIS.X, op=ALU.add)
+            nc.vector.tensor_reduce(out=total[:], in_=sc[:], axis=AXIS.X, op=ALU.add)
             weight = stage.tile([P, GROUPS], F32)
             nc.vector.reciprocal(out=weight[:], in_=total[:])
             place = (b % PAIRS_PER_BLOCK) * GROUPS
             nc.vector.tensor_tensor(
-                out=probs[:, :, place : place + GROUPS],
-                in0=scores[:].rearrange("r G m -> r m G"),
+                out=probs[block][:, :, place : place + GROUPS],
+                in0=sc[:].rearrange("r G m -> r m G"),
                 in1=weight[:].unsqueeze(1).to_broadcast([P, ROWS, GROUPS]),
                 op=ALU.mult,
             )
 
-        def array_block(block, probs):
-            second = stage.tile([P, 8, HEADS, HEADS], F32)
-            result = stage.tile([P, 8, HEADS, HEADS], F32)
+        def finish_block(block):
+            second = keep.tile([P, 8, HEADS, HEADS], F32, name="second")
+            result = keep.tile([P, 8, HEADS, HEADS], F32, name="result")
             for j in (1, 0):
                 for four in range(0, HEADS, 4):
                     back = psum_t.tile([P, 4, 8, 2, HEADS], F32, tag="flip")
                     for n in range(4):
                         nc.tensor.transpose(
                             back[:, n, :, :, :].rearrange("r e j a -> r (e j a)"),
-                            probs[:, HEADS * j + four + n, :],
+                            probs[block][:, HEADS * j + four + n, :],
                             ident[:],
                         )
                     wanted = back[:, :, :, j, :].rearrange("r h e a -> r e a h")
@@ -261,45 +275,54 @@ def tile_differentialattention_pa_t_kernel(
                         )
             nc.sync.dma_start(out=out_array[block], in_=result[:].rearrange("r e a h -> r (e a h)"))
 
-        def lane_tile(x_mx, slot, result):
-            heads = {}
+        heads = {}
+        sums = {}
+        lane_out = keep.tile([P, LANE_TILES, HEADS * HEADS], F32)
+
+        def lane_project(c):
+            if c % 2 == 0:
+                quantise_two_tiles(PAIRS + c // 2)
             for role in ("q", "k"):
-                heads[role] = stage.tile([P, D, ROWS], F32, name="heads_" + role)
+                heads[c, role] = stage.tile([P, D, ROWS], F32, name="heads_" + role)
                 for half in range(2):
-                    y = project(x_mx, slot, role, half)
+                    y = project(2 * PAIRS + c, role, half)
                     nc.scalar.activation(
-                        out=heads[role][:].rearrange("p d (j h) -> p d j h", j=2)[
+                        out=heads[c, role][:].rearrange("p d (j h) -> p d j h", j=2)[
                             :, :, :, 4 * half : 4 * half + 4
                         ],
                         in_=y[:].rearrange("p (h d j) -> p d j h", h=4, j=2),
                         func=FUNC.Copy,
                         scale=SCALE if role == "q" else 1.0,
                     )
-            sums = [psum_s.tile([P, P], F32, name="sums_%d" % j) for j in range(2)]
+
+        def lane_chunk(c, d0):
+            if d0 == 0:
+                sums[c] = [psum_s.tile([P, P], F32, name="sums_%d" % j) for j in range(2)]
             shape = [P, D_CHUNK, ROWS, ROWS]
-            for d0 in range(0, D, D_CHUNK):
-                prod = prods.tile(shape, F32)
-                nc.vector.tensor_tensor(
-                    out=prod[:],
-                    in0=heads["q"][:, d0 : d0 + D_CHUNK, :].unsqueeze(3).to_broadcast(shape),
-                    in1=heads["k"][:, d0 : d0 + D_CHUNK, :].unsqueeze(2).to_broadcast(shape),
-                    op=ALU.mult,
-                )
-                flat = prod[:].rearrange("p d i m -> p d (i m)")
-                for dd in range(D_CHUNK):
-                    for j in range(2):
-                        nc.tensor.matmul(
-                            out=sums[j][:],
-                            lhsT=flat[:, dd, j * P : (j + 1) * P],
-                            rhs=ident[:],
-                            is_transpose=True,
-                            start=(d0 + dd == 0),
-                            stop=(d0 + dd == D - 1),
-                        )
+            prod = prods.tile(shape, F32)
+            nc.vector.tensor_tensor(
+                out=prod[:],
+                in0=heads[c, "q"][:, d0 : d0 + D_CHUNK, :].unsqueeze(3).to_broadcast(shape),
+                in1=heads[c, "k"][:, d0 : d0 + D_CHUNK, :].unsqueeze(2).to_broadcast(shape),
+                op=ALU.mult,
+            )
+            flat = prod[:].rearrange("p d i m -> p d (i m)")
+            for dd in range(D_CHUNK):
+                for j in range(2):
+                    nc.tensor.matmul(
+                        out=sums[c][j][:],
+                        lhsT=flat[:, dd, j * P : (j + 1) * P],
+                        rhs=ident[:],
+                        is_transpose=True,
+                        start=(d0 + dd == 0),
+                        stop=(d0 + dd == D - 1),
+                    )
+
+        def lane_finish(c):
             sums_sb = stage.tile([P, 2, P], F32)
             back = psum_t.tile([P, 2, P], F32, tag="flip")
             for j in range(2):
-                nc.scalar.copy(out=sums_sb[:, j, :], in_=sums[j][:])
+                nc.scalar.copy(out=sums_sb[:, j, :], in_=sums[c][j][:])
                 nc.tensor.transpose(back[:, j, :], sums_sb[:, j, :], ident[:])
             sc = back[:].rearrange("p j (h m) -> p (j h) m", m=ROWS)
 
@@ -335,27 +358,39 @@ def tile_differentialattention_pa_t_kernel(
                 op=ALU.mult,
             )
             nc.vector.tensor_tensor(
-                out=result.rearrange("p (a h) -> p a h", h=HEADS),
+                out=lane_out[:, c, :].rearrange("p (a h) -> p a h", h=HEADS),
                 in0=upper[:],
                 in1=lower[:],
                 op=ALU.add,
             )
 
-        probs = None
-        for t in range(ROUNDS):
-            if t + 1 < ROUNDS:
-                x_rounds.append(load_x(t + 1))
-            x_mx = quantise_round(x_rounds[t])
-            lane_out = stage.tile([P, LANE_PER_ROUND, HEADS * HEADS], F32)
-            for n in range(PAIRS_PER_ROUND):
-                b = t * PAIRS_PER_ROUND + n
-                if b % PAIRS_PER_BLOCK == 0:
-                    probs = stage.tile([P, ROWS, P], F32, name="probs")
-                array_pair(x_mx, 2 * n, b, probs)
-                if b % PAIRS_PER_BLOCK == PAIRS_PER_BLOCK - 1:
-                    array_block(b // PAIRS_PER_BLOCK, probs)
-                if n < LANE_PER_ROUND:
-                    lane_tile(x_mx, 2 * PAIRS_PER_ROUND + n, lane_out[:, n, :])
-            nc.sync.dma_start(
-                out=out_lane[:, t * LANE_PER_ROUND : (t + 1) * LANE_PER_ROUND, :], in_=lane_out[:]
-            )
+        def lane_step(chunk):
+            per_tile = D // D_CHUNK
+            c, n = divmod(chunk, per_tile)
+            if n == per_tile - LANE_AHEAD and c + 1 < LANE_TILES:
+                lane_project(c + 1)
+            lane_chunk(c, n * D_CHUNK)
+            if n == per_tile - 1:
+                lane_finish(c)
+
+        quantise_two_tiles(0)
+        lane_project(0)
+        lane_chunks_done = 0
+        for t in range(STEPS):
+            if t + 1 < PAIRS:
+                quantise_two_tiles(t + 1)
+            for quarter in range(4):
+                if t < PAIRS:
+                    project_quarter(t, quarter)
+                if 0 <= t - 1 < PAIRS:
+                    flip_quarter(t - 1, quarter)
+                if 0 <= t - 2:
+                    score_quarter(t - 2, quarter)
+                while lane_chunks_done * QUARTERS < LANE_CHUNKS * (4 * t + quarter + 1):
+                    lane_step(lane_chunks_done)
+                    lane_chunks_done += 1
+            if 0 <= t - 2:
+                softmax_pair(t - 2)
+                if (t - 2) % PAIRS_PER_BLOCK == PAIRS_PER_BLOCK - 1:
+                    finish_block((t - 2) // PAIRS_PER_BLOCK)
+        nc.sync.dma_start(out=out_lane, in_=lane_out[:])

@@ -32,8 +32,9 @@ ARRAY_TOKENS = PAIRS * 2 * P
 PAIRS_PER_BLOCK = 4
 PAIRS_PER_LOAD = 3
 GROUPS = P // 4
-D_CHUNK = 8
-LANE_CHUNKS = LANE_TILES * (D // D_CHUNK)
+D_CHUNK = 16
+CHUNKS_PER_TILE = 2 * (D // D_CHUNK)
+LANE_CHUNKS = LANE_TILES * CHUNKS_PER_TILE
 LANE_AHEAD = 4
 STEPS = PAIRS + 2
 QUARTERS = 4 * STEPS
@@ -60,6 +61,7 @@ def tile_differentialattention_pa_t_kernel(
         psum_t = ctx.enter_context(tc.psum_pool(name="psum_t", bufs=2))
         psum_c = ctx.enter_context(tc.psum_pool(name="psum_c", bufs=2))
         psum_s = ctx.enter_context(tc.psum_pool(name="psum_s", bufs=1))
+        psum_v = ctx.enter_context(tc.psum_pool(name="psum_v", bufs=1))
 
         ident = keep.tile([P, P], F32)
         make_identity(nc, ident[:])
@@ -121,7 +123,7 @@ def tile_differentialattention_pa_t_kernel(
         x_words = x_sb[:].rearrange("p c k -> p (c k)").bitcast(F32)
 
         def quantise_two_tiles(two):
-            flipped = psum_t.tile([P, 2, 2, P], F32, tag="flip")
+            flipped = psum_v.tile([P, 2, 2, P], F32, tag="for_vector")
             for e in range(2):
                 first_word = (2 * two + e) * (K // 2)
                 for u in range(2):
@@ -251,7 +253,10 @@ def tile_differentialattention_pa_t_kernel(
             result = keep.tile([P, 8, HEADS, HEADS], F32, name="result")
             for j in (1, 0):
                 for four in range(0, HEADS, 4):
-                    back = psum_t.tile([P, 4, 8, 2, HEADS], F32, tag="flip")
+                    if j == 1:
+                        back = psum_t.tile([P, 4, 8, 2, HEADS], F32, tag="flip")
+                    else:
+                        back = psum_v.tile([P, 4, 8, 2, HEADS], F32, tag="for_vector")
                     for n in range(4):
                         nc.tensor.transpose(
                             back[:, n, :, :, :].rearrange("r e j a -> r (e j a)"),
@@ -295,34 +300,41 @@ def tile_differentialattention_pa_t_kernel(
                         scale=SCALE if role == "q" else 1.0,
                     )
 
-        def lane_chunk(c, d0):
-            if d0 == 0:
-                sums[c] = [psum_s.tile([P, P], F32, name="sums_%d" % j) for j in range(2)]
-            shape = [P, D_CHUNK, ROWS, ROWS]
+        def lane_chunk(c, j, d0):
+            if j == 0 and d0 == 0:
+                sums[c] = psum_s.tile([P, 2, P], F32, name="sums")
+            shape = [P, D_CHUNK, HEADS, ROWS]
+            some_d = slice(d0, d0 + D_CHUNK)
             prod = prods.tile(shape, F32)
             nc.vector.tensor_tensor(
                 out=prod[:],
-                in0=heads[c, "q"][:, d0 : d0 + D_CHUNK, :].unsqueeze(3).to_broadcast(shape),
-                in1=heads[c, "k"][:, d0 : d0 + D_CHUNK, :].unsqueeze(2).to_broadcast(shape),
+                in0=heads[c, "q"][:, some_d, HEADS * j : HEADS * (j + 1)].unsqueeze(3).to_broadcast(shape),
+                in1=heads[c, "k"][:, some_d, :].unsqueeze(2).to_broadcast(shape),
                 op=ALU.mult,
             )
-            flat = prod[:].rearrange("p d i m -> p d (i m)")
-            for dd in range(D_CHUNK):
-                for j in range(2):
-                    nc.tensor.matmul(
-                        out=sums[c][j][:],
-                        lhsT=flat[:, dd, j * P : (j + 1) * P],
-                        rhs=ident[:],
-                        is_transpose=True,
-                        start=(d0 + dd == 0),
-                        stop=(d0 + dd == D - 1),
-                    )
+            fold = D_CHUNK // 2
+            nc.vector.tensor_tensor(
+                out=prod[:, 0:fold, :, :],
+                in0=prod[:, 0:fold, :, :],
+                in1=prod[:, fold:D_CHUNK, :, :],
+                op=ALU.add,
+            )
+            flat = prod[:].rearrange("p d h m -> p d (h m)")
+            for dd in range(fold):
+                nc.tensor.matmul(
+                    out=sums[c][:, j, :],
+                    lhsT=flat[:, dd, :],
+                    rhs=ident[:],
+                    is_transpose=True,
+                    start=(d0 + dd == 0),
+                    stop=(d0 + D_CHUNK == D and dd == fold - 1),
+                )
 
         def lane_finish(c):
             sums_sb = stage.tile([P, 2, P], F32)
-            back = psum_t.tile([P, 2, P], F32, tag="flip")
+            back = psum_v.tile([P, 2, P], F32, tag="for_vector")
+            nc.scalar.copy(out=sums_sb[:], in_=sums[c][:])
             for j in range(2):
-                nc.scalar.copy(out=sums_sb[:, j, :], in_=sums[c][j][:])
                 nc.tensor.transpose(back[:, j, :], sums_sb[:, j, :], ident[:])
             sc = back[:].rearrange("p j (h m) -> p (j h) m", m=ROWS)
 
@@ -365,12 +377,12 @@ def tile_differentialattention_pa_t_kernel(
             )
 
         def lane_step(chunk):
-            per_tile = D // D_CHUNK
-            c, n = divmod(chunk, per_tile)
-            if n == per_tile - LANE_AHEAD and c + 1 < LANE_TILES:
+            c, n = divmod(chunk, CHUNKS_PER_TILE)
+            if n == CHUNKS_PER_TILE - LANE_AHEAD and c + 1 < LANE_TILES:
                 lane_project(c + 1)
-            lane_chunk(c, n * D_CHUNK)
-            if n == per_tile - 1:
+            j, part = divmod(n, D // D_CHUNK)
+            lane_chunk(c, j, part * D_CHUNK)
+            if n == CHUNKS_PER_TILE - 1:
                 lane_finish(c)
 
         quantise_two_tiles(0)

@@ -25,12 +25,13 @@ BANK = 512
 SCALE = D ** -0.5
 LAM_INIT = 0.8 - 0.6 * math.exp(-0.3 * 12)
 
-TILES = TOKENS // P
-PAIRS = 12
-LANE_TILES = TILES - 2 * PAIRS
-ARRAY_TOKENS = PAIRS * 2 * P
+PAIRS = 13
+LAST_QUARTERS = 2
+ARRAY_TOKENS = (PAIRS - 1) * 2 * P + LAST_QUARTERS * 2 * P // 4
+LANE_TILES = (TOKENS - ARRAY_TOKENS) // P
+TILES = 2 * PAIRS + LANE_TILES
 PAIRS_PER_BLOCK = 4
-PAIRS_PER_LOAD = 3
+LOADS = ((0, 3), (3, 3), (6, 3), (9, 4))
 GROUPS = P // 4
 D_CHUNK = 16
 CHUNKS_PER_TILE = 2 * (D // D_CHUNK)
@@ -48,8 +49,8 @@ def tile_differentialattention_pa_t_kernel(
     nc = tc.nc
     x_flat = x.flatten_outer_dims()
     out_flat = out.rearrange("b n a h -> (b n) (a h)")
-    x_array = x_flat[0:ARRAY_TOKENS, :].rearrange("(b p s) k -> p b (s k)", p=P, s=2)
-    out_array = out_flat[0:ARRAY_TOKENS, :].rearrange("(B r e) f -> B r (e f)", r=P, e=8)
+    x_array = x_flat[0 : PAIRS * 2 * P, :].rearrange("(b p s) k -> p b (s k)", p=P, s=2)
+    out_array = out_flat[0:ARRAY_TOKENS, :].rearrange("(r e) f -> r (e f)", e=8)
     x_lane = x_flat[ARRAY_TOKENS:TOKENS, :].rearrange("(p c) k -> p c k", c=LANE_TILES)
     out_lane = out_flat[ARRAY_TOKENS:TOKENS, :].rearrange("(p c) f -> p c f", c=LANE_TILES)
 
@@ -74,15 +75,15 @@ def tile_differentialattention_pa_t_kernel(
             w_planes[role] = keep.tile([P, DIM], U8, name="w_planes_" + role, align_bytes=64)
             nc.vector.memset(w_planes[role][:].bitcast(I32), 0)
 
-        def load_pairs(first_pair):
-            pairs = slice(first_pair, first_pair + PAIRS_PER_LOAD)
-            tiles = slice(2 * first_pair, 2 * (first_pair + PAIRS_PER_LOAD))
+        def load_pairs(first_pair, count):
+            pairs = slice(first_pair, first_pair + count)
+            tiles = slice(2 * first_pair, 2 * (first_pair + count))
             nc.sync.dma_start(
                 out=x_sb[:, tiles, :].rearrange("p (b s) k -> p b (s k)", s=2),
                 in_=x_array[:, pairs, :],
             )
 
-        load_pairs(0)
+        load_pairs(LOADS[0][0], LOADS[0][1])
         for role, words, scales in (("q", Wq_words, Wq_scales), ("k", Wk_words, Wk_scales)):
             nc.sync.dma_start(
                 out=w_words[role][:].bitcast(I32),
@@ -94,8 +95,8 @@ def tile_differentialattention_pa_t_kernel(
                     in_=scales[0, 4 * quadrant : 4 * quadrant + 4, :].bitcast(I32),
                 )
         nc.sync.dma_start(out=x_sb[:, 2 * PAIRS : TILES, :], in_=x_lane)
-        for first_pair in range(PAIRS_PER_LOAD, PAIRS, PAIRS_PER_LOAD):
-            load_pairs(first_pair)
+        for first_pair, count in LOADS[1:]:
+            load_pairs(first_pair, count)
 
         lam_vecs = keep.tile([P, 4, D], BF16)
         for n, vec in enumerate((lq1, lq2, lk1, lk2)):
@@ -118,13 +119,14 @@ def tile_differentialattention_pa_t_kernel(
         for n in range(2):
             nc.gpsimd.memset(queries[n][:], 0.0)
 
-        x_codes = keep.tile([P, TOKENS], U32, align_bytes=64)
-        x_planes = keep.tile([P, TOKENS], U8, align_bytes=64)
+        x_codes = keep.tile([P, TILES * P], U32, align_bytes=64)
+        x_planes = keep.tile([P, TILES * P], U8, align_bytes=64)
         x_words = x_sb[:].rearrange("p c k -> p (c k)").bitcast(F32)
 
         def quantise_two_tiles(two):
+            count = min(2, TILES - 2 * two)
             flipped = psum_v.tile([P, 2, 2, P], F32, tag="for_vector")
-            for e in range(2):
+            for e in range(count):
                 first_word = (2 * two + e) * (K // 2)
                 for u in range(2):
                     nc.tensor.transpose(
@@ -134,12 +136,14 @@ def tile_differentialattention_pa_t_kernel(
                     )
             grouped = stage.tile([P, 2 * P * 4], BF16, align_bytes=64)
             nc.vector.tensor_copy(
-                out=grouped[:].bitcast(F32).rearrange("p (e t u) -> p e t u", e=2, u=2),
-                in_=flipped[:].rearrange("p e u t -> p e t u"),
+                out=grouped[:, 0 : count * P * 4].bitcast(F32).rearrange("p (e t u) -> p e t u", e=count, u=2),
+                in_=flipped[:, 0:count, :, :].rearrange("p e u t -> p e t u"),
             )
-            cols = slice(2 * two * P, 2 * (two + 1) * P)
+            cols = slice(2 * two * P, (2 * two + count) * P)
             nc.vector.quantize_mx(
-                out=x_codes[:, cols].bitcast(FP8X4), scales=x_planes[:, cols], in_=grouped[:]
+                out=x_codes[:, cols].bitcast(FP8X4),
+                scales=x_planes[:, cols],
+                in_=grouped[:, 0 : count * P * 4],
             )
 
         def project(c, role, half):
@@ -160,7 +164,10 @@ def tile_differentialattention_pa_t_kernel(
         rows = {}
         keys = {}
         scores = {}
-        probs = {}
+        probs = keep.tile([P, ROWS, P], F32, name="probs")
+
+        def groups_of(b):
+            return GROUPS if b < PAIRS - 1 else LAST_QUARTERS * GROUPS // 4
 
         def project_quarter(b, quarter):
             s, role = quarter // 2, ("q", "k")[quarter % 2]
@@ -223,32 +230,30 @@ def tile_differentialattention_pa_t_kernel(
                 )
 
         def softmax_pair(b):
-            block = b // PAIRS_PER_BLOCK
-            if b % PAIRS_PER_BLOCK == 0:
-                probs[block] = keep.tile([P, ROWS, P], F32, name="probs")
-            sc = scores[b]
+            groups = groups_of(b)
+            sc = scores[b][:, 0:groups, :]
             top = stage.tile([P, GROUPS], F32)
-            nc.vector.tensor_reduce(out=top[:], in_=sc[:], axis=AXIS.X, op=ALU.max)
+            nc.vector.tensor_reduce(out=top[:, 0:groups], in_=sc, axis=AXIS.X, op=ALU.max)
             nc.vector.tensor_tensor(
-                out=sc[:],
-                in0=sc[:],
-                in1=top[:].unsqueeze(2).to_broadcast([P, GROUPS, ROWS]),
+                out=sc,
+                in0=sc,
+                in1=top[:, 0:groups].unsqueeze(2).to_broadcast([P, groups, ROWS]),
                 op=ALU.subtract,
             )
-            nc.scalar.activation(out=sc[:], in_=sc[:], func=FUNC.Exp)
+            nc.scalar.activation(out=sc, in_=sc, func=FUNC.Exp)
             total = stage.tile([P, GROUPS], F32)
-            nc.vector.tensor_reduce(out=total[:], in_=sc[:], axis=AXIS.X, op=ALU.add)
+            nc.vector.tensor_reduce(out=total[:, 0:groups], in_=sc, axis=AXIS.X, op=ALU.add)
             weight = stage.tile([P, GROUPS], F32)
-            nc.vector.reciprocal(out=weight[:], in_=total[:])
+            nc.vector.reciprocal(out=weight[:, 0:groups], in_=total[:, 0:groups])
             place = (b % PAIRS_PER_BLOCK) * GROUPS
             nc.vector.tensor_tensor(
-                out=probs[block][:, :, place : place + GROUPS],
-                in0=sc[:].rearrange("r G m -> r m G"),
-                in1=weight[:].unsqueeze(1).to_broadcast([P, ROWS, GROUPS]),
+                out=probs[:, :, place : place + groups],
+                in0=sc.rearrange("r G m -> r m G"),
+                in1=weight[:, 0:groups].unsqueeze(1).to_broadcast([P, ROWS, groups]),
                 op=ALU.mult,
             )
 
-        def finish_block(block):
+        def finish_block(block, used):
             second = keep.tile([P, 8, HEADS, HEADS], F32, name="second")
             result = keep.tile([P, 8, HEADS, HEADS], F32, name="result")
             for j in (1, 0):
@@ -260,7 +265,7 @@ def tile_differentialattention_pa_t_kernel(
                     for n in range(4):
                         nc.tensor.transpose(
                             back[:, n, :, :, :].rearrange("r e j a -> r (e j a)"),
-                            probs[block][:, HEADS * j + four + n, :],
+                            probs[:, HEADS * j + four + n, :],
                             ident[:],
                         )
                     wanted = back[:, :, :, j, :].rearrange("r h e a -> r e a h")
@@ -278,7 +283,10 @@ def tile_differentialattention_pa_t_kernel(
                             in1=second[:, :, :, four : four + 4],
                             op=ALU.add,
                         )
-            nc.sync.dma_start(out=out_array[block], in_=result[:].rearrange("r e a h -> r (e a h)"))
+            nc.sync.dma_start(
+                out=out_array[block * P : block * P + used, :],
+                in_=result[0:used, :, :, :].rearrange("r e a h -> r (e a h)"),
+            )
 
         heads = {}
         sums = {}
@@ -396,13 +404,15 @@ def tile_differentialattention_pa_t_kernel(
                     project_quarter(t, quarter)
                 if 0 <= t - 1 < PAIRS:
                     flip_quarter(t - 1, quarter)
-                if 0 <= t - 2:
+                if 0 <= t - 2 and 8 * quarter < groups_of(t - 2):
                     score_quarter(t - 2, quarter)
                 while lane_chunks_done * QUARTERS < LANE_CHUNKS * (4 * t + quarter + 1):
                     lane_step(lane_chunks_done)
                     lane_chunks_done += 1
             if 0 <= t - 2:
                 softmax_pair(t - 2)
-                if (t - 2) % PAIRS_PER_BLOCK == PAIRS_PER_BLOCK - 1:
-                    finish_block((t - 2) // PAIRS_PER_BLOCK)
+                if (t - 2) % PAIRS_PER_BLOCK == PAIRS_PER_BLOCK - 1 or t - 2 == PAIRS - 1:
+                    finish_block(
+                        (t - 2) // PAIRS_PER_BLOCK, (t - 2) % PAIRS_PER_BLOCK * GROUPS + groups_of(t - 2)
+                    )
         nc.sync.dma_start(out=out_lane, in_=lane_out[:])

@@ -37,7 +37,8 @@ D_CHUNK = 16
 CHUNKS_PER_TILE = 2 * (D // D_CHUNK)
 LANE_CHUNKS = LANE_TILES * CHUNKS_PER_TILE
 LANE_AHEAD = 4
-STEPS = PAIRS + 2
+STEPS = PAIRS + 1
+PADDED = (2 * ROWS + 1) * D
 QUARTERS = 4 * STEPS
 
 FLOPS = 2 * TOKENS * K * 2 * DIM + 2 * TOKENS * ROWS * ROWS * D
@@ -58,8 +59,8 @@ def tile_differentialattention_pa_t_kernel(
         keep = ctx.enter_context(tc.tile_pool(name="keep", bufs=1))
         stage = ctx.enter_context(tc.tile_pool(name="stage", bufs=2))
         prods = ctx.enter_context(tc.tile_pool(name="prods", bufs=4))
-        psum_y = ctx.enter_context(tc.psum_pool(name="psum_y", bufs=2))
-        psum_t = ctx.enter_context(tc.psum_pool(name="psum_t", bufs=2))
+        psum_y = ctx.enter_context(tc.psum_pool(name="psum_y", bufs=3))
+        psum_t = ctx.enter_context(tc.psum_pool(name="psum_t", bufs=1))
         psum_c = ctx.enter_context(tc.psum_pool(name="psum_c", bufs=2))
         psum_s = ctx.enter_context(tc.psum_pool(name="psum_s", bufs=1))
         psum_v = ctx.enter_context(tc.psum_pool(name="psum_v", bufs=1))
@@ -98,6 +99,26 @@ def tile_differentialattention_pa_t_kernel(
         for first_pair, count in LOADS[1:]:
             load_pairs(first_pair, count)
 
+        padded_words = {}
+        padded_planes = {}
+        for role in ("q", "k"):
+            padded_words[role] = keep.tile([P, PADDED], U32, name="padded_words_" + role, align_bytes=64)
+            padded_planes[role] = keep.tile([P, PADDED], U8, name="padded_planes_" + role, align_bytes=64)
+            nc.vector.memset(padded_words[role][:].bitcast(I32), 0)
+            nc.vector.memset(padded_planes[role][:].bitcast(I32), 0)
+            nc.vector.tensor_copy(
+                out=padded_words[role][:, D:PADDED].bitcast(I32).rearrange(
+                    "p (j h z d) -> p j h z d", j=2, h=HEADS, z=2
+                )[:, :, :, 0, :],
+                in_=w_words[role][:].bitcast(I32).rearrange("p (h d j) -> p j h d", h=HEADS, j=2),
+            )
+            nc.vector.tensor_copy(
+                out=padded_planes[role][:, D:PADDED].rearrange(
+                    "p (j h z d) -> p j h z d", j=2, h=HEADS, z=2
+                )[:, :, :, 0, :].rearrange("p j h d -> p h d j"),
+                in_=w_planes[role][:].rearrange("p (h d j) -> p h d j", h=HEADS, j=2),
+            )
+
         lam_vecs = keep.tile([P, 4, D], BF16)
         for n, vec in enumerate((lq1, lq2, lk1, lk2)):
             nc.scalar.dma_start(out=lam_vecs[:, n, :], in_=vec.partition_broadcast(P))
@@ -114,10 +135,6 @@ def tile_differentialattention_pa_t_kernel(
             out=neg_lam[:], in0=lam_exps[:, 1:2], in1=lam_exps[:, 0:1], op=ALU.subtract
         )
         nc.vector.tensor_scalar_add(out=neg_lam[:], in0=neg_lam[:], scalar1=-LAM_INIT)
-
-        queries = [keep.tile([P, P, 2, ROWS], F32, name="queries_%d" % n) for n in range(2)]
-        for n in range(2):
-            nc.gpsimd.memset(queries[n][:], 0.0)
 
         x_codes = keep.tile([P, TILES * P], U32, align_bytes=64)
         x_planes = keep.tile([P, TILES * P], U8, align_bytes=64)
@@ -161,53 +178,51 @@ def tile_differentialattention_pa_t_kernel(
             )
             return y
 
-        rows = {}
         keys = {}
+        queries = {}
         scores = {}
         probs = keep.tile([P, ROWS, P], F32, name="probs")
 
         def groups_of(b):
             return GROUPS if b < PAIRS - 1 else LAST_QUARTERS * GROUPS // 4
 
-        def project_quarter(b, quarter):
-            s, role = quarter // 2, ("q", "k")[quarter % 2]
-            if s == 0:
-                rows[b, role] = stage.tile([P, ROWS, 2, D], F32, name="rows_" + role)
-            for half in range(2):
-                y = project(2 * b + s, role, half)
-                nc.scalar.activation(
-                    out=rows[b, role][:].rearrange("p (j h) s d -> p j h s d", j=2)[
-                        :, :, 4 * half : 4 * half + 4, s, :
-                    ],
-                    in_=y[:].rearrange("p (h d j) -> p j h d", h=4, j=2),
-                    func=FUNC.Copy,
-                    scale=SCALE if role == "q" else 1.0,
+        def head_row(bank, n, role, i, b, sides):
+            for s in sides:
+                first = D * (2 * i + 1 - s)
+                tokens = slice((2 * b + s) * P, (2 * b + s + 1) * P)
+                nc.tensor.matmul_mx(
+                    out=bank[:, n, :],
+                    lhsT=padded_words[role][:, first : first + P].bitcast(FP8X4),
+                    lhsT_scale=padded_planes[role][:, first : first + P],
+                    rhs=x_codes[:, tokens].bitcast(FP8X4),
+                    rhs_scale=x_planes[:, tokens],
+                    start=(s == sides[0]),
+                    stop=(s == sides[-1]),
                 )
 
-        def flip_quarter(b, quarter):
-            role = ("k", "q")[quarter // 2]
+        def make_quarter(b, quarter):
             if quarter == 0:
                 keys[b] = stage.tile([P, P, ROWS], F32, name="keys")
-            for four in range(8 * (quarter % 2), 8 * (quarter % 2) + 8, 4):
-                flipped = psum_t.tile([P, 4, P], F32, tag="flip")
+                queries[b] = stage.tile([P, P, 2, ROWS], F32, name="queries")
+            four = 4 * quarter
+            used = 4 * groups_of(b)
+            bank = psum_y.tile([P, 4, P], F32, name="y")
+            for n in range(4):
+                head_row(bank, n, "k", four + n, b, (0, 1))
+            nc.scalar.copy(
+                out=keys[b][:, 0:used, four : four + 4],
+                in_=bank[:, :, 0:used].rearrange("r n p -> r p n"),
+            )
+            for s in range(2):
+                bank = psum_y.tile([P, 4, P], F32, name="y")
                 for n in range(4):
-                    nc.tensor.transpose(
-                        flipped[:, n, :],
-                        rows[b, role][:, four + n, :, :].rearrange("p s d -> p (s d)"),
-                        ident[:],
-                    )
-                if role == "k":
-                    nc.scalar.copy(
-                        out=keys[b][:, :, four : four + 4],
-                        in_=flipped[:].rearrange("r n p -> r p n"),
-                    )
-                else:
-                    for s in range(2):
-                        own = slice(D * s, D * (s + 1))
-                        nc.scalar.copy(
-                            out=queries[b % 2][own, :, s, four : four + 4],
-                            in_=flipped[own, :, :].rearrange("r n p -> r p n"),
-                        )
+                    head_row(bank, n, "q", four + n, b, (s,))
+                nc.scalar.activation(
+                    out=queries[b][:, 0:used, s, four : four + 4],
+                    in_=bank[:, :, 0:used].rearrange("r n p -> r p n"),
+                    func=FUNC.Copy,
+                    scale=SCALE,
+                )
 
         def score_quarter(b, quarter):
             if quarter == 0:
@@ -218,7 +233,7 @@ def tile_differentialattention_pa_t_kernel(
                 four_p = slice(4 * (first + n), 4 * (first + n + 1))
                 nc.tensor.matmul(
                     out=cross[:, n, :, :],
-                    lhsT=queries[b % 2][:, four_p, :, :].rearrange("r p s i -> r (p s i)"),
+                    lhsT=queries[b][:, four_p, :, :].rearrange("r p s i -> r (p s i)"),
                     rhs=keys[b][:, four_p, :],
                     start=True,
                     stop=True,
@@ -401,18 +416,16 @@ def tile_differentialattention_pa_t_kernel(
                 quantise_two_tiles(t + 1)
             for quarter in range(4):
                 if t < PAIRS:
-                    project_quarter(t, quarter)
-                if 0 <= t - 1 < PAIRS:
-                    flip_quarter(t - 1, quarter)
-                if 0 <= t - 2 and 8 * quarter < groups_of(t - 2):
-                    score_quarter(t - 2, quarter)
+                    make_quarter(t, quarter)
+                if 0 <= t - 1 and 8 * quarter < groups_of(t - 1):
+                    score_quarter(t - 1, quarter)
                 while lane_chunks_done * QUARTERS < LANE_CHUNKS * (4 * t + quarter + 1):
                     lane_step(lane_chunks_done)
                     lane_chunks_done += 1
-            if 0 <= t - 2:
-                softmax_pair(t - 2)
-                if (t - 2) % PAIRS_PER_BLOCK == PAIRS_PER_BLOCK - 1 or t - 2 == PAIRS - 1:
+            if 0 <= t - 1:
+                softmax_pair(t - 1)
+                if (t - 1) % PAIRS_PER_BLOCK == PAIRS_PER_BLOCK - 1 or t - 1 == PAIRS - 1:
                     finish_block(
-                        (t - 2) // PAIRS_PER_BLOCK, (t - 2) % PAIRS_PER_BLOCK * GROUPS + groups_of(t - 2)
+                        (t - 1) // PAIRS_PER_BLOCK, (t - 1) % PAIRS_PER_BLOCK * GROUPS + groups_of(t - 1)
                     )
         nc.sync.dma_start(out=out_lane, in_=lane_out[:])

@@ -26,16 +26,18 @@ SCALE = D ** -0.5
 LAM_INIT = 0.8 - 0.6 * math.exp(-0.3 * 12)
 
 PAIRS = 13
-LAST_QUARTERS = 2
+LAST_QUARTERS = 3
 ARRAY_TOKENS = (PAIRS - 1) * 2 * P + LAST_QUARTERS * 2 * P // 4
-LANE_TILES = (TOKENS - ARRAY_TOKENS) // P
+FULL_LANES = (TOKENS - ARRAY_TOKENS) // P
+LANE_TILES = FULL_LANES + 1
+HALF = P // 2
 TILES = 2 * PAIRS + LANE_TILES
 PAIRS_PER_BLOCK = 4
 LOADS = ((0, 3), (3, 3), (6, 3), (9, 4))
 GROUPS = P // 4
 D_CHUNK = 16
 CHUNKS_PER_TILE = 2 * (D // D_CHUNK)
-LANE_CHUNKS = LANE_TILES * CHUNKS_PER_TILE
+LANE_CHUNKS = FULL_LANES * CHUNKS_PER_TILE + CHUNKS_PER_TILE // 2
 LANE_AHEAD = 4
 STEPS = PAIRS + 1
 PADDED = (2 * ROWS + 1) * D
@@ -52,8 +54,9 @@ def tile_differentialattention_pa_t_kernel(
     out_flat = out.rearrange("b n a h -> (b n) (a h)")
     x_array = x_flat[0 : PAIRS * 2 * P, :].rearrange("(b p s) k -> p b (s k)", p=P, s=2)
     out_array = out_flat[0:ARRAY_TOKENS, :].rearrange("(r e) f -> r (e f)", e=8)
-    x_lane = x_flat[ARRAY_TOKENS:TOKENS, :].rearrange("(p c) k -> p c k", c=LANE_TILES)
-    out_lane = out_flat[ARRAY_TOKENS:TOKENS, :].rearrange("(p c) f -> p c f", c=LANE_TILES)
+    last = ARRAY_TOKENS + FULL_LANES * P
+    x_lane = x_flat[ARRAY_TOKENS:last, :].rearrange("(p c) k -> p c k", c=FULL_LANES)
+    out_lane = out_flat[ARRAY_TOKENS:last, :].rearrange("(p c) f -> p c f", c=FULL_LANES)
 
     with ExitStack() as ctx:
         keep = ctx.enter_context(tc.tile_pool(name="keep", bufs=1))
@@ -95,7 +98,11 @@ def tile_differentialattention_pa_t_kernel(
                     out=w_planes[role][32 * quadrant : 32 * quadrant + 4, :].bitcast(I32),
                     in_=scales[0, 4 * quadrant : 4 * quadrant + 4, :].bitcast(I32),
                 )
-        nc.sync.dma_start(out=x_sb[:, 2 * PAIRS : TILES, :], in_=x_lane)
+        nc.sync.dma_start(out=x_sb[:, 2 * PAIRS : TILES - 1, :], in_=x_lane)
+        for side in range(2):
+            nc.sync.dma_start(
+                out=x_sb[HALF * side : HALF * (side + 1), TILES - 1, :], in_=x_flat[last:TOKENS, :]
+            )
         for first_pair, count in LOADS[1:]:
             load_pairs(first_pair, count)
 
@@ -307,6 +314,9 @@ def tile_differentialattention_pa_t_kernel(
         sums = {}
         lane_out = keep.tile([P, LANE_TILES, HEADS * HEADS], F32)
 
+        def depth(c):
+            return D if c < FULL_LANES else D // 2
+
         def lane_project(c):
             if c % 2 == 0:
                 quantise_two_tiles(PAIRS + c // 2)
@@ -314,14 +324,20 @@ def tile_differentialattention_pa_t_kernel(
                 heads[c, role] = stage.tile([P, D, ROWS], F32, name="heads_" + role)
                 for half in range(2):
                     y = project(2 * PAIRS + c, role, half)
-                    nc.scalar.activation(
-                        out=heads[c, role][:].rearrange("p d (j h) -> p d j h", j=2)[
-                            :, :, :, 4 * half : 4 * half + 4
-                        ],
-                        in_=y[:].rearrange("p (h d j) -> p d j h", h=4, j=2),
-                        func=FUNC.Copy,
-                        scale=SCALE if role == "q" else 1.0,
-                    )
+                    for rows, first_d in ((slice(0, P), 0),) if c < FULL_LANES else (
+                        (slice(0, HALF), 0),
+                        (slice(HALF, P), depth(c)),
+                    ):
+                        nc.scalar.activation(
+                            out=heads[c, role][:].rearrange("p d (j h) -> p d j h", j=2)[
+                                rows, 0 : depth(c), :, 4 * half : 4 * half + 4
+                            ],
+                            in_=y[:].rearrange("p (h d j) -> p d j h", h=4, j=2)[
+                                rows, first_d : first_d + depth(c), :, :
+                            ],
+                            func=FUNC.Copy,
+                            scale=SCALE if role == "q" else 1.0,
+                        )
 
         def lane_chunk(c, j, d0):
             if j == 0 and d0 == 0:
@@ -350,13 +366,20 @@ def tile_differentialattention_pa_t_kernel(
                     rhs=ident[:],
                     is_transpose=True,
                     start=(d0 + dd == 0),
-                    stop=(d0 + D_CHUNK == D and dd == fold - 1),
+                    stop=(d0 + D_CHUNK == depth(c) and dd == fold - 1),
                 )
 
         def lane_finish(c):
             sums_sb = stage.tile([P, 2, P], F32)
             back = psum_v.tile([P, 2, P], F32, tag="for_vector")
             nc.scalar.copy(out=sums_sb[:], in_=sums[c][:])
+            if c == FULL_LANES:
+                nc.vector.tensor_tensor(
+                    out=sums_sb[:, :, 0:HALF],
+                    in0=sums_sb[:, :, 0:HALF],
+                    in1=sums_sb[:, :, HALF:P],
+                    op=ALU.add,
+                )
             for j in range(2):
                 nc.tensor.transpose(back[:, j, :], sums_sb[:, j, :], ident[:])
             sc = back[:].rearrange("p j (h m) -> p (j h) m", m=ROWS)
@@ -401,11 +424,12 @@ def tile_differentialattention_pa_t_kernel(
 
         def lane_step(chunk):
             c, n = divmod(chunk, CHUNKS_PER_TILE)
-            if n == CHUNKS_PER_TILE - LANE_AHEAD and c + 1 < LANE_TILES:
+            chunks = 2 * (depth(c) // D_CHUNK)
+            if n == max(chunks - LANE_AHEAD, 0) and c + 1 < LANE_TILES:
                 lane_project(c + 1)
-            j, part = divmod(n, D // D_CHUNK)
+            j, part = divmod(n, depth(c) // D_CHUNK)
             lane_chunk(c, j, part * D_CHUNK)
-            if n == CHUNKS_PER_TILE - 1:
+            if n == chunks - 1:
                 lane_finish(c)
 
         quantise_two_tiles(0)
@@ -428,4 +452,5 @@ def tile_differentialattention_pa_t_kernel(
                     finish_block(
                         (t - 1) // PAIRS_PER_BLOCK, (t - 1) % PAIRS_PER_BLOCK * GROUPS + groups_of(t - 1)
                     )
-        nc.sync.dma_start(out=out_lane, in_=lane_out[:])
+        nc.sync.dma_start(out=out_lane, in_=lane_out[:, 0:FULL_LANES, :])
+        nc.sync.dma_start(out=out_flat[last:TOKENS, :], in_=lane_out[0:HALF, FULL_LANES, :])

@@ -61,6 +61,7 @@ def tile_differentialattention_pa_t_kernel(
     with ExitStack() as ctx:
         keep = ctx.enter_context(tc.tile_pool(name="keep", bufs=1))
         stage = ctx.enter_context(tc.tile_pool(name="stage", bufs=2))
+        three = ctx.enter_context(tc.tile_pool(name="three", bufs=3))
         prods = ctx.enter_context(tc.tile_pool(name="prods", bufs=4))
         psum_y = ctx.enter_context(tc.psum_pool(name="psum_y", bufs=3))
         psum_t = ctx.enter_context(tc.psum_pool(name="psum_t", bufs=1))
@@ -145,9 +146,10 @@ def tile_differentialattention_pa_t_kernel(
 
         x_codes = keep.tile([P, TILES * P], U32, align_bytes=64)
         x_planes = keep.tile([P, TILES * P], U8, align_bytes=64)
+        grouped = {}
         x_words = x_sb[:].rearrange("p c k -> p (c k)").bitcast(F32)
 
-        def quantise_two_tiles(two):
+        def group_two_tiles(two):
             count = min(2, TILES - 2 * two)
             flipped = psum_v.tile([P, 2, 2, P], F32, tag="for_vector")
             for e in range(count):
@@ -158,16 +160,19 @@ def tile_differentialattention_pa_t_kernel(
                         x_words[:, first_word + u : first_word + K // 2 : 2],
                         ident[:],
                     )
-            grouped = stage.tile([P, 2 * P * 4], BF16, align_bytes=64)
+            grouped[two] = stage.tile([P, 2 * P * 4], BF16, name="grouped", align_bytes=64)
             nc.vector.tensor_copy(
-                out=grouped[:, 0 : count * P * 4].bitcast(F32).rearrange("p (e t u) -> p e t u", e=count, u=2),
+                out=grouped[two][:, 0 : count * P * 4].bitcast(F32).rearrange("p (e t u) -> p e t u", e=count, u=2),
                 in_=flipped[:, 0:count, :, :].rearrange("p e u t -> p e t u"),
             )
+
+        def quantise_two_tiles(two):
+            count = min(2, TILES - 2 * two)
             cols = slice(2 * two * P, (2 * two + count) * P)
             nc.vector.quantize_mx(
                 out=x_codes[:, cols].bitcast(FP8X4),
                 scales=x_planes[:, cols],
-                in_=grouped[:, 0 : count * P * 4],
+                in_=grouped[two][:, 0 : count * P * 4],
             )
 
         def project(c, role, half):
@@ -233,7 +238,7 @@ def tile_differentialattention_pa_t_kernel(
 
         def score_quarter(b, quarter):
             if quarter == 0:
-                scores[b] = stage.tile([P, GROUPS, ROWS], F32, name="scores")
+                scores[b] = three.tile([P, GROUPS, ROWS], F32, name="scores")
             first = 8 * quarter
             cross = psum_c.tile([P, 8, 4, ROWS], F32)
             for n in range(8):
@@ -254,26 +259,40 @@ def tile_differentialattention_pa_t_kernel(
         def softmax_pair(b):
             groups = groups_of(b)
             sc = scores[b][:, 0:groups, :]
-            top = stage.tile([P, GROUPS], F32)
-            nc.vector.tensor_reduce(out=top[:, 0:groups], in_=sc, axis=AXIS.X, op=ALU.max)
-            nc.vector.tensor_tensor(
-                out=sc,
-                in0=sc,
-                in1=top[:, 0:groups].unsqueeze(2).to_broadcast([P, groups, ROWS]),
-                op=ALU.subtract,
-            )
-            nc.scalar.activation(out=sc, in_=sc, func=FUNC.Exp)
-            total = stage.tile([P, GROUPS], F32)
-            nc.vector.tensor_reduce(out=total[:, 0:groups], in_=sc, axis=AXIS.X, op=ALU.add)
-            weight = stage.tile([P, GROUPS], F32)
-            nc.vector.reciprocal(out=weight[:, 0:groups], in_=total[:, 0:groups])
+            top = three.tile([P, GROUPS], F32, name="top")
+            total = three.tile([P, GROUPS], F32, name="total")
+            weight = three.tile([P, GROUPS], F32, name="weight")
             place = (b % PAIRS_PER_BLOCK) * GROUPS
-            nc.vector.tensor_tensor(
-                out=probs[:, :, place : place + groups],
-                in0=sc.rearrange("r G m -> r m G"),
-                in1=weight[:, 0:groups].unsqueeze(1).to_broadcast([P, ROWS, groups]),
-                op=ALU.mult,
-            )
+
+            def maximum():
+                nc.vector.tensor_reduce(out=top[:, 0:groups], in_=sc, axis=AXIS.X, op=ALU.max)
+
+            def exponential():
+                nc.vector.tensor_tensor(
+                    out=sc,
+                    in0=sc,
+                    in1=top[:, 0:groups].unsqueeze(2).to_broadcast([P, groups, ROWS]),
+                    op=ALU.subtract,
+                )
+                nc.scalar.activation(out=sc, in_=sc, func=FUNC.Exp)
+
+            def add_up():
+                nc.vector.tensor_reduce(out=total[:, 0:groups], in_=sc, axis=AXIS.X, op=ALU.add)
+
+            def invert():
+                nc.vector.reciprocal(out=weight[:, 0:groups], in_=total[:, 0:groups])
+
+            def divide():
+                nc.vector.tensor_tensor(
+                    out=probs[:, :, place : place + groups].rearrange("r (m i) G -> r m G i", i=4),
+                    in0=sc.rearrange("r G (m i) -> r m G i", i=4),
+                    in1=weight[:, 0:groups].unsqueeze(1).unsqueeze(3).to_broadcast([P, ROWS // 4, groups, 4]),
+                    op=ALU.mult,
+                )
+                if b % PAIRS_PER_BLOCK == PAIRS_PER_BLOCK - 1 or b == PAIRS - 1:
+                    finish_block(b // PAIRS_PER_BLOCK, place + groups)
+
+            return [maximum, exponential, add_up, invert, divide]
 
         def finish_block(block, used):
             second = keep.tile([P, 8, HEADS, HEADS], F32, name="second")
@@ -311,6 +330,7 @@ def tile_differentialattention_pa_t_kernel(
             )
 
         heads = {}
+        products = {}
         sums = {}
         lane_out = keep.tile([P, LANE_TILES, HEADS * HEADS], F32)
 
@@ -318,8 +338,6 @@ def tile_differentialattention_pa_t_kernel(
             return D if c < FULL_LANES else D // 2
 
         def lane_project(c):
-            if c % 2 == 0:
-                quantise_two_tiles(PAIRS + c // 2)
             for role in ("q", "k"):
                 heads[c, role] = stage.tile([P, D, ROWS], F32, name="heads_" + role)
                 for half in range(2):
@@ -339,18 +357,21 @@ def tile_differentialattention_pa_t_kernel(
                             scale=SCALE if role == "q" else 1.0,
                         )
 
-        def lane_chunk(c, j, d0):
-            if j == 0 and d0 == 0:
-                sums[c] = psum_s.tile([P, 2, P], F32, name="sums")
+        def lane_multiply(c, j, d0):
             shape = [P, D_CHUNK, HEADS, ROWS]
             some_d = slice(d0, d0 + D_CHUNK)
-            prod = prods.tile(shape, F32)
+            products[c, j, d0] = prods.tile(shape, F32, name="prod")
             nc.vector.tensor_tensor(
-                out=prod[:],
+                out=products[c, j, d0][:],
                 in0=heads[c, "q"][:, some_d, HEADS * j : HEADS * (j + 1)].unsqueeze(3).to_broadcast(shape),
                 in1=heads[c, "k"][:, some_d, :].unsqueeze(2).to_broadcast(shape),
                 op=ALU.mult,
             )
+
+        def lane_sum(c, j, d0):
+            if j == 0 and d0 == 0:
+                sums[c] = psum_s.tile([P, 2, P], F32, name="sums")
+            prod = products[c, j, d0]
             fold = D_CHUNK // 2
             nc.vector.tensor_tensor(
                 out=prod[:, 0:fold, :, :],
@@ -370,87 +391,132 @@ def tile_differentialattention_pa_t_kernel(
                 )
 
         def lane_finish(c):
-            sums_sb = stage.tile([P, 2, P], F32)
-            back = psum_v.tile([P, 2, P], F32, tag="for_vector")
-            nc.scalar.copy(out=sums_sb[:], in_=sums[c][:])
-            if c == FULL_LANES:
-                nc.vector.tensor_tensor(
-                    out=sums_sb[:, :, 0:HALF],
-                    in0=sums_sb[:, :, 0:HALF],
-                    in1=sums_sb[:, :, HALF:P],
-                    op=ALU.add,
-                )
-            for j in range(2):
-                nc.tensor.transpose(back[:, j, :], sums_sb[:, j, :], ident[:])
-            sc = back[:].rearrange("p j (h m) -> p (j h) m", m=ROWS)
-
             square = [P, ROWS, ROWS]
             corner = [P, HEADS, HEADS]
-            peak = stage.tile([P, ROWS], F32)
-            nc.vector.tensor_reduce(out=peak[:], in_=sc, axis=AXIS.X, op=ALU.max)
-            expd = stage.tile(square, F32)
-            nc.vector.tensor_tensor(
-                out=expd[:], in0=sc, in1=peak[:].unsqueeze(2).to_broadcast(square), op=ALU.subtract
-            )
-            nc.scalar.activation(out=expd[:], in_=expd[:], func=FUNC.Exp)
-            norm = stage.tile([P, ROWS], F32)
-            nc.vector.tensor_reduce(out=norm[:], in_=expd[:], axis=AXIS.X, op=ALU.add)
-            inverse = stage.tile([P, ROWS], F32)
-            nc.vector.reciprocal(out=inverse[:], in_=norm[:])
-            minus = stage.tile([P, HEADS], F32)
-            nc.vector.tensor_scalar_mul(
-                out=minus[:], in0=inverse[:, HEADS:ROWS], scalar1=neg_lam[:, 0:1]
-            )
-            upper = stage.tile(corner, F32)
-            nc.vector.tensor_tensor(
-                out=upper[:],
-                in0=expd[:, 0:HEADS, 0:HEADS],
-                in1=inverse[:, 0:HEADS].unsqueeze(2).to_broadcast(corner),
-                op=ALU.mult,
-            )
-            lower = stage.tile(corner, F32)
-            nc.vector.tensor_tensor(
-                out=lower[:],
-                in0=expd[:, HEADS:ROWS, HEADS:ROWS],
-                in1=minus[:].unsqueeze(2).to_broadcast(corner),
-                op=ALU.mult,
-            )
-            nc.vector.tensor_tensor(
-                out=lane_out[:, c, :].rearrange("p (a h) -> p a h", h=HEADS),
-                in0=upper[:],
-                in1=lower[:],
-                op=ALU.add,
-            )
+            sums_sb = stage.tile([P, 2, P], F32, name="sums_sb")
+            lane_sc = stage.tile([P, 2, P], F32, name="lane_sc")
+            peak = stage.tile([P, ROWS], F32, name="peak")
+            expd = stage.tile(square, F32, name="expd")
+            norm = stage.tile([P, ROWS], F32, name="norm")
+            inverse = stage.tile([P, ROWS], F32, name="inverse")
+            minus = stage.tile([P, HEADS], F32, name="minus")
+            upper = stage.tile(corner, F32, name="upper")
+            lower = stage.tile(corner, F32, name="lower")
+            sc = lane_sc[:].rearrange("p j (h m) -> p (j h) m", m=ROWS)
+
+            def turn():
+                nc.scalar.copy(out=sums_sb[:], in_=sums[c][:])
+                if c == FULL_LANES:
+                    nc.vector.tensor_tensor(
+                        out=sums_sb[:, :, 0:HALF],
+                        in0=sums_sb[:, :, 0:HALF],
+                        in1=sums_sb[:, :, HALF:P],
+                        op=ALU.add,
+                    )
+                back = psum_v.tile([P, 2, P], F32, tag="for_vector")
+                for j in range(2):
+                    nc.tensor.transpose(back[:, j, :], sums_sb[:, j, :], ident[:])
+                nc.scalar.copy(out=lane_sc[:], in_=back[:])
+
+            def maximum():
+                nc.vector.tensor_reduce(out=peak[:], in_=sc, axis=AXIS.X, op=ALU.max)
+
+            def exponential():
+                nc.vector.tensor_tensor(
+                    out=expd[:], in0=sc, in1=peak[:].unsqueeze(2).to_broadcast(square), op=ALU.subtract
+                )
+                nc.scalar.activation(out=expd[:], in_=expd[:], func=FUNC.Exp)
+
+            def add_up():
+                nc.vector.tensor_reduce(out=norm[:], in_=expd[:], axis=AXIS.X, op=ALU.add)
+
+            def invert():
+                nc.vector.reciprocal(out=inverse[:], in_=norm[:])
+
+            def divide():
+                nc.vector.tensor_scalar_mul(
+                    out=minus[:], in0=inverse[:, HEADS:ROWS], scalar1=neg_lam[:, 0:1]
+                )
+                nc.vector.tensor_tensor(
+                    out=upper[:],
+                    in0=expd[:, 0:HEADS, 0:HEADS],
+                    in1=inverse[:, 0:HEADS].unsqueeze(2).to_broadcast(corner),
+                    op=ALU.mult,
+                )
+                nc.vector.tensor_tensor(
+                    out=lower[:],
+                    in0=expd[:, HEADS:ROWS, HEADS:ROWS],
+                    in1=minus[:].unsqueeze(2).to_broadcast(corner),
+                    op=ALU.mult,
+                )
+
+            def subtract():
+                nc.vector.tensor_tensor(
+                    out=lane_out[:, c, :].rearrange("p (a h) -> p a h", h=HEADS),
+                    in0=upper[:],
+                    in1=lower[:],
+                    op=ALU.add,
+                )
+
+            return [turn, maximum, exponential, add_up, invert, divide, subtract]
+
+        stages = []
+
+        def next_stages():
+            for some in list(stages):
+                some[0]()
+                some.remove(some[0])
+                if not some:
+                    stages.remove(some)
 
         def lane_step(chunk):
             c, n = divmod(chunk, CHUNKS_PER_TILE)
             chunks = 2 * (depth(c) // D_CHUNK)
             if n == max(chunks - LANE_AHEAD, 0) and c + 1 < LANE_TILES:
                 lane_project(c + 1)
-            j, part = divmod(n, depth(c) // D_CHUNK)
-            lane_chunk(c, j, part * D_CHUNK)
-            if n == chunks - 1:
-                lane_finish(c)
+            if n == 0 and c % 2 == 1 and c + 1 < LANE_TILES:
+                two = PAIRS + (c + 1) // 2
+                group_two_tiles(two)
+                stages.append([lambda: quantise_two_tiles(two)])
+            lane_multiply(*place_of(chunk))
+            next_stages()
+            if chunk > 0:
+                lane_close(chunk - 1)
 
-        quantise_two_tiles(0)
+        def place_of(chunk):
+            c, n = divmod(chunk, CHUNKS_PER_TILE)
+            j, part = divmod(n, depth(c) // D_CHUNK)
+            return c, j, part * D_CHUNK
+
+        def lane_close(chunk):
+            c, j, d0 = place_of(chunk)
+            lane_sum(c, j, d0)
+            if j == 1 and d0 + D_CHUNK == depth(c):
+                stages.append(lane_finish(c))
+
+        for two in (0, PAIRS):
+            group_two_tiles(two)
+            quantise_two_tiles(two)
         lane_project(0)
         lane_chunks_done = 0
         for t in range(STEPS):
-            if t + 1 < PAIRS:
-                quantise_two_tiles(t + 1)
             for quarter in range(4):
                 if t < PAIRS:
                     make_quarter(t, quarter)
+                if quarter == 0 and t + 1 < PAIRS:
+                    group_two_tiles(t + 1)
+                if quarter == 1 and t + 1 < PAIRS:
+                    quantise_two_tiles(t + 1)
                 if 0 <= t - 1 and 8 * quarter < groups_of(t - 1):
                     score_quarter(t - 1, quarter)
                 while lane_chunks_done * QUARTERS < LANE_CHUNKS * (4 * t + quarter + 1):
                     lane_step(lane_chunks_done)
                     lane_chunks_done += 1
+                    if lane_chunks_done == LANE_CHUNKS:
+                        lane_close(LANE_CHUNKS - 1)
             if 0 <= t - 1:
-                softmax_pair(t - 1)
-                if (t - 1) % PAIRS_PER_BLOCK == PAIRS_PER_BLOCK - 1 or t - 1 == PAIRS - 1:
-                    finish_block(
-                        (t - 1) // PAIRS_PER_BLOCK, (t - 1) % PAIRS_PER_BLOCK * GROUPS + groups_of(t - 1)
-                    )
+                stages.append(softmax_pair(t - 1))
+        while stages:
+            next_stages()
         nc.sync.dma_start(out=out_lane, in_=lane_out[:, 0:FULL_LANES, :])
         nc.sync.dma_start(out=out_flat[last:TOKENS, :], in_=lane_out[0:HALF, FULL_LANES, :])

import math
from contextlib import ExitStack

import concourse.mybir as mybir
from concourse.masks import make_identity

FP8X4 = mybir.dt.float8_e4m3fn_x4
BF16 = mybir.dt.bfloat16
F32 = mybir.dt.float32
I32 = mybir.dt.int32
U32 = mybir.dt.uint32
U8 = mybir.dt.uint8
ALU = mybir.AluOpType
FUNC = mybir.ActivationFunctionType
AXIS = mybir.AxisListType

P = 128
TOKENS = 4096
K = 512
DIM = 1024
HEADS = 8
D = 64
ROWS = 2 * HEADS
BANK = 512
SCALE = D ** -0.5
LAM_INIT = 0.8 - 0.6 * math.exp(-0.3 * 12)

PAIRS = 13
LAST_QUARTERS = 3
ARRAY_TOKENS = (PAIRS - 1) * 2 * P + LAST_QUARTERS * 2 * P // 4
FULL_LANES = (TOKENS - ARRAY_TOKENS) // P
LANE_TILES = FULL_LANES + 1
HALF = P // 2
TILES = 2 * PAIRS + LANE_TILES
PAIRS_PER_BLOCK = 4
LOADS = ((0, 3), (3, 3), (6, 3), (9, 4))
GROUPS = P // 4
D_CHUNK = 16
CHUNKS_PER_TILE = 2 * (D // D_CHUNK)
LANE_CHUNKS = FULL_LANES * CHUNKS_PER_TILE + CHUNKS_PER_TILE // 2
LANE_AHEAD = 4
STEPS = PAIRS + 1
PADDED = (2 * ROWS + 1) * D
QUARTERS = 4 * STEPS

FLOPS = 2 * TOKENS * K * 2 * DIM + 2 * TOKENS * ROWS * ROWS * D


def tile_differentialattention_pa_t_kernel(
    tc, x, Wq_words, Wq_scales, Wk_words, Wk_scales, lq1, lq2, lk1, lk2, out
):
    nc = tc.nc
    x_flat = x.flatten_outer_dims()
    out_flat = out.rearrange("b n a h -> (b n) (a h)")
    x_array = x_flat[0 : PAIRS * 2 * P, :].rearrange("(b p s) k -> p b (s k)", p=P, s=2)
    out_array = out_flat[0:ARRAY_TOKENS, :].rearrange("(r e) f -> r (e f)", e=8)
    last = ARRAY_TOKENS + FULL_LANES * P
    x_lane = x_flat[ARRAY_TOKENS:last, :].rearrange("(p c) k -> p c k", c=FULL_LANES)
    out_lane = out_flat[ARRAY_TOKENS:last, :].rearrange("(p c) f -> p c f", c=FULL_LANES)

    with ExitStack() as ctx:
        keep = ctx.enter_context(tc.tile_pool(name="keep", bufs=1))
        stage = ctx.enter_context(tc.tile_pool(name="stage", bufs=2))
        three = ctx.enter_context(tc.tile_pool(name="three", bufs=3))
        prods = ctx.enter_context(tc.tile_pool(name="prods", bufs=4))
        psum_y = ctx.enter_context(tc.psum_pool(name="psum_y", bufs=3))
        psum_t = ctx.enter_context(tc.psum_pool(name="psum_t", bufs=1))
        psum_c = ctx.enter_context(tc.psum_pool(name="psum_c", bufs=2))
        psum_s = ctx.enter_context(tc.psum_pool(name="psum_s", bufs=1))
        psum_v = ctx.enter_context(tc.psum_pool(name="psum_v", bufs=1))

        ident = keep.tile([P, P], F32)
        make_identity(nc, ident[:])

        x_sb = keep.tile([P, TILES, K], BF16)
        w_words = {}
        w_planes = {}
        for role in ("q", "k"):
            w_words[role] = keep.tile([P, DIM], U32, name="w_words_" + role, align_bytes=64)
            w_planes[role] = keep.tile([P, DIM], U8, name="w_planes_" + role, align_bytes=64)
            nc.vector.memset(w_planes[role][:].bitcast(I32), 0)

        def load_pairs(first_pair, count):
            pairs = slice(first_pair, first_pair + count)
            tiles = slice(2 * first_pair, 2 * (first_pair + count))
            nc.sync.dma_start(
                out=x_sb[:, tiles, :].rearrange("p (b s) k -> p b (s k)", s=2),
                in_=x_array[:, pairs, :],
            )

        load_pairs(LOADS[0][0], LOADS[0][1])
        for role, words, scales in (("q", Wq_words, Wq_scales), ("k", Wk_words, Wk_scales)):
            nc.sync.dma_start(
                out=w_words[role][:].bitcast(I32),
                in_=words[0].rearrange("p n t -> p (n t)").bitcast(I32),
            )
            for quadrant in range(4):
                nc.sync.dma_start(
                    out=w_planes[role][32 * quadrant : 32 * quadrant + 4, :].bitcast(I32),
                    in_=scales[0, 4 * quadrant : 4 * quadrant + 4, :].bitcast(I32),
                )
        nc.sync.dma_start(out=x_sb[:, 2 * PAIRS : TILES - 1, :], in_=x_lane)
        for side in range(2):
            nc.sync.dma_start(
                out=x_sb[HALF * side : HALF * (side + 1), TILES - 1, :], in_=x_flat[last:TOKENS, :]
            )
        for first_pair, count in LOADS[1:]:
            load_pairs(first_pair, count)

        padded_words = {}
        padded_planes = {}
        for role in ("q", "k"):
            padded_words[role] = keep.tile([P, PADDED], U32, name="padded_words_" + role, align_bytes=64)
            padded_planes[role] = keep.tile([P, PADDED], U8, name="padded_planes_" + role, align_bytes=64)
            nc.vector.memset(padded_words[role][:].bitcast(I32), 0)
            nc.vector.memset(padded_planes[role][:].bitcast(I32), 0)
            nc.vector.tensor_copy(
                out=padded_words[role][:, D:PADDED].bitcast(I32).rearrange(
                    "p (j h z d) -> p j h z d", j=2, h=HEADS, z=2
                )[:, :, :, 0, :],
                in_=w_words[role][:].bitcast(I32).rearrange("p (h d j) -> p j h d", h=HEADS, j=2),
            )
            nc.vector.tensor_copy(
                out=padded_planes[role][:, D:PADDED].rearrange(
                    "p (j h z d) -> p j h z d", j=2, h=HEADS, z=2
                )[:, :, :, 0, :].rearrange("p j h d -> p h d j"),
                in_=w_planes[role][:].rearrange("p (h d j) -> p h d j", h=HEADS, j=2),
            )

        lam_vecs = keep.tile([P, 4, D], BF16)
        for n, vec in enumerate((lq1, lq2, lk1, lk2)):
            nc.scalar.dma_start(out=lam_vecs[:, n, :], in_=vec.partition_broadcast(P))
        lam_prod = keep.tile([P, 2, D], F32)
        nc.vector.tensor_tensor(
            out=lam_prod[:], in0=lam_vecs[:, 0:2, :], in1=lam_vecs[:, 2:4, :], op=ALU.mult
        )
        lam_dots = keep.tile([P, 2], F32)
        nc.vector.tensor_reduce(out=lam_dots[:], in_=lam_prod[:], axis=AXIS.X, op=ALU.add)
        lam_exps = keep.tile([P, 2], F32)
        nc.scalar.activation(out=lam_exps[:], in_=lam_dots[:], func=FUNC.Exp)
        neg_lam = keep.tile([P, 1], F32)
        nc.vector.tensor_tensor(
            out=neg_lam[:], in0=lam_exps[:, 1:2], in1=lam_exps[:, 0:1], op=ALU.subtract
        )
        nc.vector.tensor_scalar_add(out=neg_lam[:], in0=neg_lam[:], scalar1=-LAM_INIT)

        x_codes = keep.tile([P, TILES * P], U32, align_bytes=64)
        x_planes = keep.tile([P, TILES * P], U8, align_bytes=64)
        grouped = {}
        x_words = x_sb[:].rearrange("p c k -> p (c k)").bitcast(F32)

        def group_two_tiles(two):
            count = min(2, TILES - 2 * two)
            flipped = psum_v.tile([P, 2, 2, P], F32, tag="for_vector")
            for e in range(count):
                first_word = (2 * two + e) * (K // 2)
                for u in range(2):
                    nc.tensor.transpose(
                        flipped[:, e, u, :],
                        x_words[:, first_word + u : first_word + K // 2 : 2],
                        ident[:],
                    )
            grouped[two] = stage.tile([P, 2 * P * 4], BF16, name="grouped", align_bytes=64)
            nc.vector.tensor_copy(
                out=grouped[two][:, 0 : count * P * 4].bitcast(F32).rearrange("p (e t u) -> p e t u", e=count, u=2),
                in_=flipped[:, 0:count, :, :].rearrange("p e u t -> p e t u"),
            )

        def quantise_two_tiles(two):
            count = min(2, TILES - 2 * two)
            cols = slice(2 * two * P, (2 * two + count) * P)
            nc.vector.quantize_mx(
                out=x_codes[:, cols].bitcast(FP8X4),
                scales=x_planes[:, cols],
                in_=grouped[two][:, 0 : count * P * 4],
            )

        def project(c, role, half):
            tokens = slice(c * P, (c + 1) * P)
            cols = slice(half * BANK, (half + 1) * BANK)
            y = psum_y.tile([P, BANK], F32, name="y")
            nc.tensor.matmul_mx(
                out=y[:],
                lhsT=x_codes[:, tokens].bitcast(FP8X4),
                lhsT_scale=x_planes[:, tokens],
                rhs=w_words[role][:, cols].bitcast(FP8X4),
                rhs_scale=w_planes[role][:, cols],
                start=True,
                stop=True,
            )
            return y

        keys = {}
        queries = {}
        scores = {}
        probs = keep.tile([P, ROWS, P], F32, name="probs")

        def groups_of(b):
            return GROUPS if b < PAIRS - 1 else LAST_QUARTERS * GROUPS // 4

        def head_row(bank, n, role, i, b, sides):
            for s in sides:
                first = D * (2 * i + 1 - s)
                tokens = slice((2 * b + s) * P, (2 * b + s + 1) * P)
                nc.tensor.matmul_mx(
                    out=bank[:, n, :],
                    lhsT=padded_words[role][:, first : first + P].bitcast(FP8X4),
                    lhsT_scale=padded_planes[role][:, first : first + P],
                    rhs=x_codes[:, tokens].bitcast(FP8X4),
                    rhs_scale=x_planes[:, tokens],
                    start=(s == sides[0]),
                    stop=(s == sides[-1]),
                )

        def make_quarter(b, quarter):
            if quarter == 0:
                keys[b] = stage.tile([P, P, ROWS], F32, name="keys")
                queries[b] = stage.tile([P, P, 2, ROWS], F32, name="queries")
            four = 4 * quarter
            used = 4 * groups_of(b)
            bank = psum_y.tile([P, 4, P], F32, name="y")
            for n in range(4):
                head_row(bank, n, "k", four + n, b, (0, 1))
            nc.scalar.copy(
                out=keys[b][:, 0:used, four : four + 4],
                in_=bank[:, :, 0:used].rearrange("r n p -> r p n"),
            )
            for s in range(2):
                bank = psum_y.tile([P, 4, P], F32, name="y")
                for n in range(4):
                    head_row(bank, n, "q", four + n, b, (s,))
                nc.scalar.activation(
                    out=queries[b][:, 0:used, s, four : four + 4],
                    in_=bank[:, :, 0:used].rearrange("r n p -> r p n"),
                    func=FUNC.Copy,
                    scale=SCALE,
                )

        def score_quarter(b, quarter):
            if quarter == 0:
                scores[b] = three.tile([P, GROUPS, ROWS], F32, name="scores")
            first = 8 * quarter
            cross = psum_c.tile([P, 8, 4, ROWS], F32)
            for n in range(8):
                four_p = slice(4 * (first + n), 4 * (first + n + 1))
                nc.tensor.matmul(
                    out=cross[:, n, :, :],
                    lhsT=queries[b][:, four_p, :, :].rearrange("r p s i -> r (p s i)"),
                    rhs=keys[b][:, four_p, :],
                    start=True,
                    stop=True,
                )
            for g in range(4):
                quadrant = slice(32 * g, 32 * (g + 1))
                nc.scalar.copy(
                    out=scores[b][quadrant, first : first + 8, :], in_=cross[quadrant, :, g, :]
                )

        def softmax_pair(b):
            groups = groups_of(b)
            sc = scores[b][:, 0:groups, :]
            top = three.tile([P, GROUPS], F32, name="top")
            total = three.tile([P, GROUPS], F32, name="total")
            weight = three.tile([P, GROUPS], F32, name="weight")
            place = (b % PAIRS_PER_BLOCK) * GROUPS

            def maximum():
                nc.vector.tensor_reduce(out=top[:, 0:groups], in_=sc, axis=AXIS.X, op=ALU.max)

            def exponential():
                nc.vector.tensor_tensor(
                    out=sc,
                    in0=sc,
                    in1=top[:, 0:groups].unsqueeze(2).to_broadcast([P, groups, ROWS]),
                    op=ALU.subtract,
                )
                nc.scalar.activation(out=sc, in_=sc, func=FUNC.Exp)

            def add_up():
                nc.vector.tensor_reduce(out=total[:, 0:groups], in_=sc, axis=AXIS.X, op=ALU.add)

            def invert():
                nc.vector.reciprocal(out=weight[:, 0:groups], in_=total[:, 0:groups])

            def divide():
                nc.vector.tensor_tensor(
                    out=probs[:, :, place : place + groups].rearrange("r (m i) G -> r m G i", i=4),
                    in0=sc.rearrange("r G (m i) -> r m G i", i=4),
                    in1=weight[:, 0:groups].unsqueeze(1).unsqueeze(3).to_broadcast([P, ROWS // 4, groups, 4]),
                    op=ALU.mult,
                )
                if b % PAIRS_PER_BLOCK == PAIRS_PER_BLOCK - 1 or b == PAIRS - 1:
                    finish_block(b // PAIRS_PER_BLOCK, place + groups)

            return [maximum, exponential, add_up, invert, divide]

        def finish_block(block, used):
            second = keep.tile([P, 8, HEADS, HEADS], F32, name="second")
            result = keep.tile([P, 8, HEADS, HEADS], F32, name="result")
            for j in (1, 0):
                for four in range(0, HEADS, 4):
                    if j == 1:
                        back = psum_t.tile([P, 4, 8, 2, HEADS], F32, tag="flip")
                    else:
                        back = psum_v.tile([P, 4, 8, 2, HEADS], F32, tag="for_vector")
                    for n in range(4):
                        nc.tensor.transpose(
                            back[:, n, :, :, :].rearrange("r e j a -> r (e j a)"),
                            probs[:, HEADS * j + four + n, :],
                            ident[:],
                        )
                    wanted = back[:, :, :, j, :].rearrange("r h e a -> r e a h")
                    if j == 1:
                        nc.scalar.activation(
                            out=second[:, :, :, four : four + 4],
                            in_=wanted,
                            func=FUNC.Copy,
                            scale=neg_lam[:, 0:1],
                        )
                    else:
                        nc.vector.tensor_tensor(
                            out=result[:, :, :, four : four + 4],
                            in0=wanted,
                            in1=second[:, :, :, four : four + 4],
                            op=ALU.add,
                        )
            nc.sync.dma_start(
                out=out_array[block * P : block * P + used, :],
                in_=result[0:used, :, :, :].rearrange("r e a h -> r (e a h)"),
            )

        heads = {}
        products = {}
        sums = {}
        lane_out = keep.tile([P, LANE_TILES, HEADS * HEADS], F32)

        def depth(c):
            return D if c < FULL_LANES else D // 2

        def lane_project(c):
            for role in ("q", "k"):
                heads[c, role] = stage.tile([P, D, ROWS], F32, name="heads_" + role)
                for half in range(2):
                    y = project(2 * PAIRS + c, role, half)
                    for rows, first_d in ((slice(0, P), 0),) if c < FULL_LANES else (
                        (slice(0, HALF), 0),
                        (slice(HALF, P), depth(c)),
                    ):
                        nc.scalar.activation(
                            out=heads[c, role][:].rearrange("p d (j h) -> p d j h", j=2)[
                                rows, 0 : depth(c), :, 4 * half : 4 * half + 4
                            ],
                            in_=y[:].rearrange("p (h d j) -> p d j h", h=4, j=2)[
                                rows, first_d : first_d + depth(c), :, :
                            ],
                            func=FUNC.Copy,
                            scale=SCALE if role == "q" else 1.0,
                        )

        def lane_multiply(c, j, d0):
            shape = [P, D_CHUNK, HEADS, ROWS]
            some_d = slice(d0, d0 + D_CHUNK)
            products[c, j, d0] = prods.tile(shape, F32, name="prod")
            nc.vector.tensor_tensor(
                out=products[c, j, d0][:],
                in0=heads[c, "q"][:, some_d, HEADS * j : HEADS * (j + 1)].unsqueeze(3).to_broadcast(shape),
                in1=heads[c, "k"][:, some_d, :].unsqueeze(2).to_broadcast(shape),
                op=ALU.mult,
            )

        def lane_sum(c, j, d0):
            if j == 0 and d0 == 0:
                sums[c] = psum_s.tile([P, 2, P], F32, name="sums")
            prod = products[c, j, d0]
            fold = D_CHUNK // 2
            nc.vector.tensor_tensor(
                out=prod[:, 0:fold, :, :],
                in0=prod[:, 0:fold, :, :],
                in1=prod[:, fold:D_CHUNK, :, :],
                op=ALU.add,
            )
            flat = prod[:].rearrange("p d h m -> p d (h m)")
            for dd in range(fold):
                nc.tensor.matmul(
                    out=sums[c][:, j, :],
                    lhsT=flat[:, dd, :],
                    rhs=ident[:],
                    is_transpose=True,
                    start=(d0 + dd == 0),
                    stop=(d0 + D_CHUNK == depth(c) and dd == fold - 1),
                )

        def lane_finish(c):
            square = [P, ROWS, ROWS]
            corner = [P, HEADS, HEADS]
            sums_sb = stage.tile([P, 2, P], F32, name="sums_sb")
            lane_sc = stage.tile([P, 2, P], F32, name="lane_sc")
            peak = stage.tile([P, ROWS], F32, name="peak")
            expd = stage.tile(square, F32, name="expd")
            norm = stage.tile([P, ROWS], F32, name="norm")
            inverse = stage.tile([P, ROWS], F32, name="inverse")
            minus = stage.tile([P, HEADS], F32, name="minus")
            upper = stage.tile(corner, F32, name="upper")
            lower = stage.tile(corner, F32, name="lower")
            sc = lane_sc[:].rearrange("p j (h m) -> p (j h) m", m=ROWS)

            def turn():
                nc.scalar.copy(out=sums_sb[:], in_=sums[c][:])
                if c == FULL_LANES:
                    nc.vector.tensor_tensor(
                        out=sums_sb[:, :, 0:HALF],
                        in0=sums_sb[:, :, 0:HALF],
                        in1=sums_sb[:, :, HALF:P],
                        op=ALU.add,
                    )
                back = psum_v.tile([P, 2, P], F32, tag="for_vector")
                for j in range(2):
                    nc.tensor.transpose(back[:, j, :], sums_sb[:, j, :], ident[:])
                nc.scalar.copy(out=lane_sc[:], in_=back[:])

            def maximum():
                nc.vector.tensor_reduce(out=peak[:], in_=sc, axis=AXIS.X, op=ALU.max)

            def exponential():
                nc.vector.tensor_tensor(
                    out=expd[:], in0=sc, in1=peak[:].unsqueeze(2).to_broadcast(square), op=ALU.subtract
                )
                nc.scalar.activation(out=expd[:], in_=expd[:], func=FUNC.Exp)

            def add_up():
                nc.vector.tensor_reduce(out=norm[:], in_=expd[:], axis=AXIS.X, op=ALU.add)

            def invert():
                nc.vector.reciprocal(out=inverse[:], in_=norm[:])

            def divide():
                nc.vector.tensor_scalar_mul(
                    out=minus[:], in0=inverse[:, HEADS:ROWS], scalar1=neg_lam[:, 0:1]
                )
                nc.vector.tensor_tensor(
                    out=upper[:],
                    in0=expd[:, 0:HEADS, 0:HEADS],
                    in1=inverse[:, 0:HEADS].unsqueeze(2).to_broadcast(corner),
                    op=ALU.mult,
                )
                nc.vector.tensor_tensor(
                    out=lower[:],
                    in0=expd[:, HEADS:ROWS, HEADS:ROWS],
                    in1=minus[:].unsqueeze(2).to_broadcast(corner),
                    op=ALU.mult,
                )

            def subtract():
                nc.vector.tensor_tensor(
                    out=lane_out[:, c, :].rearrange("p (a h) -> p a h", h=HEADS),
                    in0=upper[:],
                    in1=lower[:],
                    op=ALU.add,
                )

            return [turn, maximum, exponential, add_up, invert, divide, subtract]

        stages = []

        def next_stages():
            for some in list(stages):
                some[0]()
                some.remove(some[0])
                if not some:
                    stages.remove(some)

        def lane_step(chunk):
            c, n = divmod(chunk, CHUNKS_PER_TILE)
            chunks = 2 * (depth(c) // D_CHUNK)
            if n == max(chunks - LANE_AHEAD, 0) and c + 1 < LANE_TILES:
                lane_project(c + 1)
            if n == 0 and c % 2 == 1 and c + 1 < LANE_TILES:
                two = PAIRS + (c + 1) // 2
                group_two_tiles(two)
                stages.append([lambda: quantise_two_tiles(two)])
            lane_multiply(*place_of(chunk))
            next_stages()
            if chunk > 0:
                lane_close(chunk - 1)

        def place_of(chunk):
            c, n = divmod(chunk, CHUNKS_PER_TILE)
            j, part = divmod(n, depth(c) // D_CHUNK)
            return c, j, part * D_CHUNK

        def lane_close(chunk):
            c, j, d0 = place_of(chunk)
            lane_sum(c, j, d0)
            if j == 1 and d0 + D_CHUNK == depth(c):
                stages.append(lane_finish(c))

        for two in (0, PAIRS):
            group_two_tiles(two)
            quantise_two_tiles(two)
        lane_project(0)
        lane_chunks_done = 0
        for t in range(STEPS):
            for quarter in range(4):
                if t < PAIRS:
                    make_quarter(t, quarter)
                if quarter == 0 and t + 1 < PAIRS:
                    group_two_tiles(t + 1)
                if quarter == 1 and t + 1 < PAIRS:
                    quantise_two_tiles(t + 1)
                if 0 <= t - 1 and 8 * quarter < groups_of(t - 1):
                    score_quarter(t - 1, quarter)
                while lane_chunks_done * QUARTERS < LANE_CHUNKS * (4 * t + quarter + 1):
                    lane_step(lane_chunks_done)
                    lane_chunks_done += 1
                    if lane_chunks_done == LANE_CHUNKS:
                        lane_close(LANE_CHUNKS - 1)
            if 0 <= t - 1:
                stages.append(softmax_pair(t - 1))
        while stages:
            next_stages()
        nc.sync.dma_start(out=out_lane, in_=lane_out[:, 0:FULL_LANES, :])
        nc.sync.dma_start(out=out_flat[last:TOKENS, :], in_=lane_out[0:HALF, FULL_LANES, :])
